import numpy as np
import ml_dtypes


def mxq(x, axis, fmt="e4m3"):
    dtype, down = {"e4m3": (ml_dtypes.float8_e4m3fn, 7), "e5m2": (ml_dtypes.float8_e5m2, 14)}[fmt]
    v = np.moveaxis(np.asarray(x, np.float32).astype(ml_dtypes.bfloat16).astype(np.float64), axis, -1)
    blocks = v.reshape(v.shape[:-1] + (-1, 32))
    amax = np.abs(blocks).max(-1, keepdims=True)
    byte = np.maximum(np.where(amax > 0, np.frexp(amax)[1] - 1 + 127, 0) - down, 1)
    scale = np.exp2(byte - 127.0)
    codes = (blocks / scale).astype(np.float32).astype(dtype).astype(np.float64)
    return np.moveaxis((codes * scale).reshape(v.shape), -1, axis)


WIDE = False


def mx_kscale(k):
    if not WIDE:
        return np.ones(k)
    levels = np.array([10, -10, 5, -5, 0])
    if k % 512:
        return np.exp2(np.random.permutation(np.resize(levels, k // 32))).repeat(32)
    a = np.empty((k // 512, 16))
    for p in range(k // 512):
        a[p, :8] = np.random.permutation(np.resize(levels, 8))
        for g in range(8):
            far = levels[np.abs(levels - a[p, g]) >= 10]
            a[p, g + 8] = far[np.random.randint(len(far))]
    return np.exp2(a.ravel()).repeat(32)


BF16 = ml_dtypes.bfloat16


def bf(x):
    return np.asarray(x, np.float32).astype(BF16)


def f64(x):
    return np.asarray(x).astype(np.float64)


B, S, D, R, C = 128, 32, 512, 16, 1024
MIN_SCALE = 1e-3
TEMPERATURE = 1.5


def softplus(v):
    return np.logaddexp(v, 0.0)


def setup_inputs():
    s = mx_kscale(D)
    return {
        "features": bf(np.random.standard_normal((B, D)) * 0.3 * s),
        "W_diag": bf(np.random.standard_normal((D, D)) * 2.0 / np.sqrt(D) / s[None, :]),
        "b_diag": bf(-4.0 + 0.2 * np.random.standard_normal(D)),
        "W_cls": bf(np.random.standard_normal((C, D)) * 3.0 / np.sqrt(D) / s[None, :]),
        "b_cls": bf(np.random.standard_normal(C) * 0.3),
        "noise_diag": bf(np.random.standard_normal((B, S, D)) * 10.0 * s),
        "lr_samples": bf(np.random.standard_normal((B, S, D)) * 0.3 * s),
    }


def reference(features, W_diag, b_diag, W_cls, b_cls, noise_diag, lr_samples):
    f = f64(features)
    z = f64(bf(mxq(f, 1, "e4m3") @ mxq(f64(W_diag), 1, "e4m3").T)) + f64(b_diag)
    diagonal_std = softplus(z) + MIN_SCALE
    samples = f64(lr_samples) + diagonal_std[:, None, :] * f64(noise_diag)
    pre_logits = f[:, None, :] + samples
    logits = (mxq(pre_logits, 2, "e4m3") @ mxq(f64(W_cls), 1, "e4m3").T) + f64(b_cls)
    return logits / TEMPERATURE

@@ -1,0 +1,343 @@
+from contextlib import ExitStack
+
+import concourse.mybir as mybir
+from concourse.masks import make_identity
+
+F32 = mybir.dt.float32
+BF16 = mybir.dt.bfloat16
+U32 = mybir.dt.uint32
+U8 = mybir.dt.uint8
+FP8X4 = mybir.dt.float8_e4m3fn_x4
+ALU = mybir.AluOpType
+ACT = mybir.ActivationFunctionType
+
+B, S, D, C = 128, 32, 512, 1024
+P = 128
+FLOPS = 2 * B * S * D * C + 2 * B * D * D
+ZBANK = BF16
+NG = 16
+GB = 8
+INV_T = 1.0 / 1.5
+LOADS = (("n", 0, 2), ("w", 0, 0), ("n", 2, 2), ("l", 0, 2), ("n", 4, 4), ("l", 2, 2), ("n", 8, 4), ("l", 4, 4), ("n", 12, 4), ("l", 8, 4), ("l", 12, 4))
+LOOP_NOISE = 8
+WARM_START = 4
+WARM_RUN = 2
+CUTS = (2, 18)
+
+
+def tile_hetxlhead_pa_kernel(tc, features, W_diag, b_diag, W_cls, b_cls, noise_diag, lr_samples, out):
+    nc = tc.nc
+    with ExitStack() as ctx:
+        keep = ctx.enter_context(tc.tile_pool(name="keep", bufs=1))
+        work = ctx.enter_context(tc.tile_pool(name="work", bufs=3))
+        psum = ctx.enter_context(tc.psum_pool(name="psum", bufs=2))
+        ctx.enter_context(tc.manual_schedule())
+
+        n_rows = noise_diag.rearrange("b s d -> (b s) d").rearrange("(j r g) d -> r j g d", r=P, g=2)
+        l_rows = lr_samples.rearrange("b s d -> (b s) d").rearrange("(j r g) d -> r j g d", r=P, g=2)
+        o_rows = out.rearrange("b s c -> (b s) c").rearrange("(j r g) c -> r j g c", r=P, g=2)
+
+        ident = keep.tile([P, P], F32, name="ident")
+        make_identity(nc, ident[:])
+        brow = keep.tile([P, C], BF16, name="brow")
+        nc.gpsimd.memset(brow[:], 0.0)
+        ones = keep.tile([P, P], BF16, name="ones")
+        nc.gpsimd.memset(ones[:], 1.0)
+        warm_in = keep.tile([P, 2], F32, name="warm_in")
+        nc.vector.memset(warm_in[:], 0.0)
+        nc.scalar.activation(out=warm_in[:, 1:2], in_=warm_in[:, 0:1], func=ACT.Exp)
+
+        f_raw = keep.tile([P, D], BF16, name="f_raw")
+        nc.sync.dma_start(out=f_raw[:], in_=features)
+        wd_rows = W_diag.rearrange("(m t) k -> m t k", t=4)
+        wd_raw = []
+        for i in range(2):
+            wd_half = keep.tile([P, 2, D], BF16, name="wd_raw%d" % i)
+            nc.sync.dma_start(out=wd_half[:], in_=wd_rows[:, 2 * i : 2 * i + 2])
+            wd_raw.append(wd_half)
+        bd = keep.tile([P, 4], BF16, name="bd")
+        nc.sync.dma_start(out=bd[:], in_=b_diag.rearrange("(p t) -> p t", t=4))
+        wc_raw = keep.tile([P, 8, D], BF16, name="wc_raw")
+        n_words = {}
+        l_words = {}
+        for li, (what, j0, n) in enumerate(LOADS):
+            if what == "w":
+                nc.sync.dma_start(out=wc_raw[:], in_=W_cls.rearrange("(a p) d -> p a d", p=P))
+                nc.sync.dma_start(out=brow[0:1, :], in_=b_cls.rearrange("(o c) -> o c", o=1))
+            else:
+                raw = keep.tile([P, n, 2, D], BF16, name="raw%d" % li)
+                rows = n_rows if what == "n" else l_rows
+                nc.sync.dma_start(out=raw[:], in_=rows[:, j0 : j0 + n])
+                for i in range(n):
+                    if what == "n":
+                        n_words[j0 + i] = raw[:, i].bitcast(F32)
+                    else:
+                        l_words[j0 + i] = raw[:, i].bitcast(F32)
+
+        dummy = psum.tile([P, P], F32, name="dummy", tag="dm", bufs=1)
+
+        def warm(n):
+            for i in range(n):
+                nc.tensor.matmul(out=dummy[:], lhsT=ident[:], rhs=ident[:], start=True, stop=True)
+
+        def transpose_words(dst, words):
+            for u in range(2):
+                nc.tensor.transpose(out=dst[:, u, :], in_=words[:, u : 256 : 2], identity=ident[:])
+
+        nT = {}
+        xns = {}
+
+        def turn_noise(j, tag, bufs):
+            xns[j] = psum.tile([P, 2, 2, P], F32, name="xn%d" % j, tag=tag, bufs=bufs)
+            for g in range(2):
+                transpose_words(xns[j][:, g], n_words[j][:, g])
+
+        def copy_noise(j, on_scalar):
+            nT[j] = keep.tile([P, 2, 2, P], F32, name="nT%d" % j)
+            if on_scalar:
+                nc.scalar.copy(out=nT[j][:], in_=xns[j][:])
+            else:
+                nc.vector.tensor_copy(out=nT[j][:], in_=xns[j][:])
+
+        warm(WARM_START)
+        xf = psum.tile([P, 2, 2, P], F32, name="xf", tag="xn", bufs=1)
+        transpose_words(xf[:, 0], f_raw[:].bitcast(F32))
+        fg = keep.tile([P, B, 4], BF16, name="fg", align_bytes=64)
+        nc.vector.tensor_copy(out=fg[:].bitcast(F32), in_=xf[:, 0].rearrange("p u b -> p b u"))
+        f_codes = keep.tile([P, B], U32, name="f_codes", align_bytes=64)
+        f_scl = keep.tile([P, B], U8, name="f_scl", align_bytes=64)
+        wd_codes = keep.tile([P, 4 * P], U32, name="wd_codes", align_bytes=64)
+        wd_scl = keep.tile([P, 4 * P], U8, name="wd_scl", align_bytes=64)
+        wdg = []
+        for i in range(2):
+            xw = psum.tile([P, 2, 2, P], F32, name="xw%d" % i, tag="lT")
+            wd_words = wd_raw[i][:].bitcast(F32)
+            for a in range(2):
+                transpose_words(xw[:, a], wd_words[:, a])
+            wdg_half = keep.tile([P, 2, P, 4], BF16, name="wdg%d" % i, align_bytes=64)
+            wdg.append(wdg_half)
+            src = xw[:].rearrange("p a u m -> p a m u")
+            if i == 0:
+                nc.vector.tensor_copy(out=wdg_half[:].bitcast(F32), in_=src)
+                nc.vector.quantize_mx(
+                    out=f_codes[:].bitcast(FP8X4), scales=f_scl[:], in_=fg[:].rearrange("p b t -> p (b t)")
+                )
+            else:
+                nc.scalar.copy(out=wdg_half[:].bitcast(F32), in_=src)
+        for i in range(2):
+            cols = slice(2 * i * P, (2 * i + 2) * P)
+            nc.vector.quantize_mx(
+                out=wd_codes[:, cols].bitcast(FP8X4), scales=wd_scl[:, cols], in_=wdg[i][:].rearrange("p t m k -> p (t m k)")
+            )
+        warm(WARM_RUN)
+        for j in range(2):
+            turn_noise(j, "o", 4)
+            copy_noise(j, True)
+        warm(WARM_RUN)
+
+        zt = psum.tile([P, 4, P], ZBANK, name="zt", tag="xn", bufs=1)
+        for t in range(4):
+            cols = slice(t * P, (t + 1) * P)
+            nc.tensor.matmul_mx(
+                out=zt[:, t, :],
+                lhsT=wd_codes[:, cols].bitcast(FP8X4),
+                lhsT_scale=wd_scl[:, cols],
+                rhs=f_codes[:].bitcast(FP8X4),
+                rhs_scale=f_scl[:],
+                start=True,
+                stop=True,
+            )
+
+        v = keep.tile([P, 4, B], F32, name="v")
+        nc.vector.tensor_tensor(out=v[:], in0=zt[:], in1=bd[:].unsqueeze(2).to_broadcast([P, 4, B]), op=ALU.add)
+        va = keep.tile([P, 4, B], F32, name="va")
+        nc.scalar.activation(out=va[:], in_=v[:], func=ACT.Abs)
+        ve = keep.tile([P, 4, B], F32, name="ve")
+        nc.scalar.activation(out=ve[:], in_=va[:], func=ACT.Exp, scale=-1.0)
+        vr = keep.tile([P, 4, B], F32, name="vr")
+        nc.vector.tensor_scalar(out=vr[:], in0=v[:], scalar1=0.0, scalar2=1e-3, op0=ALU.max, op1=ALU.add)
+        vl = keep.tile([P, 4, B], F32, name="vl")
+        std = keep.tile([P, 4, B], F32, name="std")
+
+        def finish_std(b0, b1):
+            nc.scalar.activation(out=vl[:, :, b0:b1], in_=ve[:, :, b0:b1], func=ACT.Ln, bias=1.0)
+            nc.vector.tensor_tensor(out=std[:, :, b0:b1], in0=vr[:, :, b0:b1], in1=vl[:, :, b0:b1], op=ALU.add)
+
+        wc_words = wc_raw[:].bitcast(F32)
+        wcg = keep.tile([P, 8, P, 4], BF16, name="wcg", align_bytes=64)
+        wc_codes = keep.tile([P, C], U32, name="wc_codes", align_bytes=64)
+        wc_scl = keep.tile([P, C], U8, name="wc_scl", align_bytes=64)
+        for i in range(4):
+            xc = psum.tile([P, 2, 2, P], F32, name="xc%d" % i, tag="o", bufs=4)
+            for a in range(2):
+                transpose_words(xc[:, a], wc_words[:, 2 * i + a])
+            if i % 2 == 1:
+                warm(WARM_RUN)
+            nc.vector.tensor_copy(out=wcg[:, 2 * i : 2 * i + 2].bitcast(F32), in_=xc[:].rearrange("p a u m -> p a m u"))
+            if i == 1:
+                finish_std(0, 32)
+        finish_std(32, B)
+        for h in range(2):
+            nc.vector.quantize_mx(
+                out=wc_codes[:, h * 512 : (h + 1) * 512].bitcast(FP8X4),
+                scales=wc_scl[:, h * 512 : (h + 1) * 512],
+                in_=wcg[:, 4 * h : 4 * h + 4].rearrange("p a m k -> p (a m k)"),
+            )
+        b15 = keep.tile([P, C], F32, name="b15")
+        for h in range(2):
+            pb = psum.tile([P, 512], F32, name="pb%d" % h, tag="o", bufs=4)
+            nc.tensor.matmul(out=pb[:], lhsT=ones[:], rhs=brow[:, h * 512 : (h + 1) * 512], start=True, stop=True)
+            nc.vector.tensor_scalar_mul(out=b15[:, h * 512 : (h + 1) * 512], in0=pb[:], scalar1=INV_T)
+
+        lT = {}
+        tps = {}
+        pres = {}
+        codes = {}
+        scls = {}
+        obanks = {}
+        osbs = {}
+
+        def turn_lr(j):
+            lT[j] = psum.tile([P, 2, 2, P], F32, name="lT%d" % j, tag="lT")
+            for g in range(2):
+                transpose_words(lT[j][:, g], l_words[j][:, g])
+
+        def scale_noise(j, first, last):
+            if first == 0:
+                tps[j] = work.tile([P, 4, 2, P], F32, name="tp%d" % j, tag="tp", bufs=4)
+            src = nT[j][:].bitcast(BF16).rearrange("p g u (r e) -> p g u r e", e=2)
+            for i in range(first, last):
+                bl = i // 4
+                t = i % 4
+                b = GB * j + bl
+                rr = slice(16 * bl, 16 * bl + 16)
+                nc.scalar.activation(
+                    out=tps[j][:, t, :, rr],
+                    in_=src[:, :, t // 2, rr, t % 2],
+                    func=ACT.Identity,
+                    bias=fg[:, b, t : t + 1],
+                    scale=std[:, t, b : b + 1],
+                )
+
+        def add_lr(j):
+            pre = work.tile([P, 2, P, 4], BF16, name="pre%d" % j, tag="pre", align_bytes=64)
+            pres[j] = pre
+            a = lT[j][:].bitcast(BF16).rearrange("p g u (r e) -> p g r u e", e=2)
+            c = tps[j][:].rearrange("p (u e) g r -> p g r u e", e=2)
+            o = pre[:].rearrange("p g r (u e) -> p g r u e", e=2)
+            for g in range(2):
+                nc.vector.tensor_tensor(out=o[:, g], in0=a[:, g], in1=c[:, g], op=ALU.add)
+
+        def quantize(j):
+            codes[j] = work.tile([P, 2 * P], U32, name="codes%d" % j, tag="codes", align_bytes=64)
+            scls[j] = work.tile([P, 2 * P], U8, name="scl%d" % j, tag="scl", align_bytes=64)
+            nc.vector.quantize_mx(
+                out=codes[j][:].bitcast(FP8X4), scales=scls[j][:], in_=pres[j][:].rearrange("p g r t -> p (g r t)")
+            )
+
+        def multiply(j, k):
+            g = k // 2
+            h = k % 2
+            rows = slice(g * P, (g + 1) * P)
+            cols = slice(h * 512, (h + 1) * 512)
+            ob = psum.tile([P, 512], F32, name="ob%d_%d" % (j, k), tag="o", bufs=4)
+            obanks[(j, k)] = ob
+            nc.tensor.matmul_mx(
+                out=ob[:],
+                lhsT=codes[j][:, rows].bitcast(FP8X4),
+                lhsT_scale=scls[j][:, rows],
+                rhs=wc_codes[:, cols].bitcast(FP8X4),
+                rhs_scale=wc_scl[:, cols],
+                start=True,
+                stop=True,
+            )
+
+        def empty(j, k, on_scalar):
+            if j not in osbs:
+                osbs[j] = work.tile([P, 2, C], F32, name="osb%d" % j, tag="osb", bufs=4)
+            cols = slice((k % 2) * 512, (k % 2 + 1) * 512)
+            dst = osbs[j][:, k // 2, cols]
+            if on_scalar:
+                nc.scalar.activation(out=dst, in_=obanks[(j, k)][:], func=ACT.Copy, scale=INV_T)
+                nc.gpsimd.tensor_tensor(out=dst, in0=dst, in1=b15[:, cols], op=ALU.add)
+            else:
+                nc.vector.scalar_tensor_tensor(
+                    out=dst, in0=obanks[(j, k)][:], scalar=INV_T, in1=b15[:, cols], op0=ALU.mult, op1=ALU.add
+                )
+
+        for step in range(NG + 2):
+            jw = step
+            ja = step - 1
+            je = step - 2
+            jc = step + 1
+            jn = step + 2
+            do_w = jw < NG
+            do_a = 0 <= ja < NG
+            do_e = je >= 0
+            last = je == NG - 1
+            do_c = LOOP_NOISE <= jc < NG
+            do_n = LOOP_NOISE <= jn < NG
+            if last:
+                scalar_takes = (0,)
+            elif do_c:
+                scalar_takes = (3,)
+            else:
+                scalar_takes = (1, 3)
+
+            if do_w:
+                turn_lr(jw)
+                scale_noise(jw, 0, CUTS[0])
+            if do_c:
+                copy_noise(jc, True)
+            if do_e and 1 in scalar_takes:
+                empty(je, 1, True)
+            if do_e and 0 in scalar_takes:
+                empty(je, 0, True)
+            if do_n:
+                turn_noise(jn, "xn", 1)
+            if step == 0:
+                for j in (2, 3):
+                    turn_noise(j, "o", 4)
+                warm(WARM_RUN)
+                for j in (4, 5):
+                    turn_noise(j, "o", 4)
+            if step == 1:
+                for j in (6, 7):
+                    turn_noise(j, "o", 4)
+            if step < NG + 1:
+                warm(WARM_RUN)
+            if step == 0:
+                for j in (2, 3, 4, 5):
+                    copy_noise(j, False)
+            if do_a:
+                add_lr(ja)
+            if step == 1:
+                copy_noise(6, False)
+            if do_e and 0 not in scalar_takes:
+                empty(je, 0, False)
+            if do_a:
+                quantize(ja)
+                multiply(ja, 0)
+            if step == 1:
+                copy_noise(7, False)
+            if do_e and 1 not in scalar_takes:
+                empty(je, 1, False)
+            if last:
+                nc.sync.dma_start(out=o_rows[:, je, 0], in_=osbs[je][:, 0])
+            if do_a:
+                multiply(ja, 1)
+            if do_w:
+                scale_noise(jw, CUTS[0], CUTS[1])
+            if do_e:
+                empty(je, 3, 3 in scalar_takes)
+                empty(je, 2, False)
+            if do_a:
+                multiply(ja, 2)
+                multiply(ja, 3)
+            if do_w:
+                scale_noise(jw, CUTS[1], 32)
+            if do_e:
+                if last:
+                    nc.sync.dma_start(out=o_rows[:, je, 1], in_=osbs[je][:, 1])
+                else:
+                    nc.sync.dma_start(out=o_rows[:, je], in_=osbs[je][:])

@@ -22,7 +22,7 @@ LOADS = (("n", 0, 2), ("w", 0, 0), ("n", 2, 2), ("l", 0, 2), ("n", 4, 4), ("l", 
 LOOP_NOISE = 8
 WARM_START = 4
 WARM_RUN = 2
-CUTS = (2, 18)
+CUTS = (11, 21)
 
 
 def tile_hetxlhead_pa_kernel(tc, features, W_diag, b_diag, W_cls, b_cls, noise_diag, lr_samples, out):
@@ -204,7 +204,7 @@ def tile_hetxlhead_pa_kernel(tc, features, W_diag, b_diag, W_cls, b_cls, noise_d
 
         def scale_noise(j, first, last):
             if first == 0:
-                tps[j] = work.tile([P, 4, 2, P], F32, name="tp%d" % j, tag="tp", bufs=4)
+                tps[j] = work.tile([P, 4, 2, P], F32, name="tp%d" % j, tag="tp")
             src = nT[j][:].bitcast(BF16).rearrange("p g u (r e) -> p g u r e", e=2)
             for i in range(first, last):
                 bl = i // 4
@@ -254,7 +254,7 @@ def tile_hetxlhead_pa_kernel(tc, features, W_diag, b_diag, W_cls, b_cls, noise_d
 
         def empty(j, k, on_scalar):
             if j not in osbs:
-                osbs[j] = work.tile([P, 2, C], F32, name="osb%d" % j, tag="osb", bufs=4)
+                osbs[j] = work.tile([P, 2, C], F32, name="osb%d" % j, tag="osb")
             cols = slice((k % 2) * 512, (k % 2 + 1) * 512)
             dst = osbs[j][:, k // 2, cols]
             if on_scalar:
@@ -269,31 +269,17 @@ def tile_hetxlhead_pa_kernel(tc, features, W_diag, b_diag, W_cls, b_cls, noise_d
             jw = step
             ja = step - 1
             je = step - 2
-            jc = step + 1
-            jn = step + 2
             do_w = jw < NG
             do_a = 0 <= ja < NG
             do_e = je >= 0
             last = je == NG - 1
-            do_c = LOOP_NOISE <= jc < NG
-            do_n = LOOP_NOISE <= jn < NG
-            if last:
-                scalar_takes = (0,)
-            elif do_c:
-                scalar_takes = (3,)
-            else:
-                scalar_takes = (1, 3)
+            jn = step + 2
+            loop_noise = LOOP_NOISE <= jn < NG
+            scalar_takes = (0,) if last else ((1, 3) if (je % 2 == 1 or step >= NG) else (3,))
 
             if do_w:
                 turn_lr(jw)
-                scale_noise(jw, 0, CUTS[0])
-            if do_c:
-                copy_noise(jc, True)
-            if do_e and 1 in scalar_takes:
-                empty(je, 1, True)
-            if do_e and 0 in scalar_takes:
-                empty(je, 0, True)
-            if do_n:
+            if loop_noise:
                 turn_noise(jn, "xn", 1)
             if step == 0:
                 for j in (2, 3):
@@ -306,6 +292,9 @@ def tile_hetxlhead_pa_kernel(tc, features, W_diag, b_diag, W_cls, b_cls, noise_d
                     turn_noise(j, "o", 4)
             if step < NG + 1:
                 warm(WARM_RUN)
+
+            if do_w:
+                scale_noise(jw, 0, CUTS[0])
             if step == 0:
                 for j in (2, 3, 4, 5):
                     copy_noise(j, False)
@@ -313,24 +302,27 @@ def tile_hetxlhead_pa_kernel(tc, features, W_diag, b_diag, W_cls, b_cls, noise_d
                 add_lr(ja)
             if step == 1:
                 copy_noise(6, False)
-            if do_e and 0 not in scalar_takes:
-                empty(je, 0, False)
+            if do_e:
+                empty(je, 0, 0 in scalar_takes)
             if do_a:
                 quantize(ja)
                 multiply(ja, 0)
             if step == 1:
                 copy_noise(7, False)
-            if do_e and 1 not in scalar_takes:
-                empty(je, 1, False)
-            if last:
-                nc.sync.dma_start(out=o_rows[:, je, 0], in_=osbs[je][:, 0])
+            if do_e:
+                empty(je, 1, 1 in scalar_takes)
+                if last:
+                    nc.sync.dma_start(out=o_rows[:, je, 0], in_=osbs[je][:, 0])
             if do_a:
                 multiply(ja, 1)
             if do_w:
                 scale_noise(jw, CUTS[0], CUTS[1])
             if do_e:
                 empty(je, 3, 3 in scalar_takes)
-                empty(je, 2, False)
+            if loop_noise:
+                copy_noise(jn, True)
+            if do_e:
+                empty(je, 2, 2 in scalar_takes)
             if do_a:
                 multiply(ja, 2)
                 multiply(ja, 3)

@@ -18,7 +18,7 @@ ZBANK = BF16
 NG = 16
 GB = 8
 INV_T = 1.0 / 1.5
-LOADS = (("n", 0, 2), ("w", 0, 0), ("n", 2, 2), ("l", 0, 2), ("n", 4, 4), ("l", 2, 2), ("n", 8, 4), ("l", 4, 4), ("n", 12, 4), ("l", 8, 4), ("l", 12, 4))
+LOADS = (("n", 0, 2), ("w", 0, 0), ("n", 2, 2), ("n", 4, 4), ("l", 0, 2), ("l", 2, 2), ("n", 8, 4), ("l", 4, 4), ("n", 12, 4), ("l", 8, 4), ("l", 12, 4))
 LOOP_NOISE = 8
 WARM_START = 4
 WARM_RUN = 2
@@ -40,9 +40,9 @@ def tile_hetxlhead_pa_kernel(tc, features, W_diag, b_diag, W_cls, b_cls, noise_d
         ident = keep.tile([P, P], F32, name="ident")
         make_identity(nc, ident[:])
         brow = keep.tile([P, C], BF16, name="brow")
-        nc.gpsimd.memset(brow[:], 0.0)
+        nc.vector.memset(brow[:], 0.0)
         ones = keep.tile([P, P], BF16, name="ones")
-        nc.gpsimd.memset(ones[:], 1.0)
+        nc.vector.memset(ones[:], 1.0)
         warm_in = keep.tile([P, 2], F32, name="warm_in")
         nc.vector.memset(warm_in[:], 0.0)
         nc.scalar.activation(out=warm_in[:, 1:2], in_=warm_in[:, 0:1], func=ACT.Exp)
@@ -55,6 +55,7 @@ def tile_hetxlhead_pa_kernel(tc, features, W_diag, b_diag, W_cls, b_cls, noise_d
             wd_half = keep.tile([P, 2, D], BF16, name="wd_raw%d" % i)
             nc.sync.dma_start(out=wd_half[:], in_=wd_rows[:, 2 * i : 2 * i + 2])
             wd_raw.append(wd_half)
+        nc.sync.dma_start(out=brow[0:1, :], in_=b_cls.rearrange("(o c) -> o c", o=1))
         bd = keep.tile([P, 4], BF16, name="bd")
         nc.sync.dma_start(out=bd[:], in_=b_diag.rearrange("(p t) -> p t", t=4))
         wc_raw = keep.tile([P, 8, D], BF16, name="wc_raw")
@@ -63,7 +64,6 @@ def tile_hetxlhead_pa_kernel(tc, features, W_diag, b_diag, W_cls, b_cls, noise_d
         for li, (what, j0, n) in enumerate(LOADS):
             if what == "w":
                 nc.sync.dma_start(out=wc_raw[:], in_=W_cls.rearrange("(a p) d -> p a d", p=P))
-                nc.sync.dma_start(out=brow[0:1, :], in_=b_cls.rearrange("(o c) -> o c", o=1))
             else:
                 raw = keep.tile([P, n, 2, D], BF16, name="raw%d" % li)
                 rows = n_rows if what == "n" else l_rows
@@ -129,7 +129,11 @@ def tile_hetxlhead_pa_kernel(tc, features, W_diag, b_diag, W_cls, b_cls, noise_d
             nc.vector.quantize_mx(
                 out=wd_codes[:, cols].bitcast(FP8X4), scales=wd_scl[:, cols], in_=wdg[i][:].rearrange("p t m k -> p (t m k)")
             )
-        warm(WARM_RUN)
+        b15 = keep.tile([P, C], F32, name="b15")
+        for h in range(2):
+            pb = psum.tile([P, 512], F32, name="pb%d" % h, tag="o", bufs=4)
+            nc.tensor.matmul(out=pb[:], lhsT=ones[:], rhs=brow[:, h * 512 : (h + 1) * 512], start=True, stop=True)
+            nc.scalar.activation(out=b15[:, h * 512 : (h + 1) * 512], in_=pb[:], func=ACT.Copy, scale=INV_T)
         for j in range(2):
             turn_noise(j, "o", 4)
             copy_noise(j, True)
@@ -148,14 +152,13 @@ def tile_hetxlhead_pa_kernel(tc, features, W_diag, b_diag, W_cls, b_cls, noise_d
                 stop=True,
             )
 
-        v = keep.tile([P, 4, B], F32, name="v")
-        nc.vector.tensor_tensor(out=v[:], in0=zt[:], in1=bd[:].unsqueeze(2).to_broadcast([P, 4, B]), op=ALU.add)
         va = keep.tile([P, 4, B], F32, name="va")
-        nc.scalar.activation(out=va[:], in_=v[:], func=ACT.Abs)
+        for t in range(4):
+            nc.scalar.activation(out=va[:, t, :], in_=zt[:, t, :], func=ACT.Abs, bias=bd[:, t : t + 1])
         ve = keep.tile([P, 4, B], F32, name="ve")
         nc.scalar.activation(out=ve[:], in_=va[:], func=ACT.Exp, scale=-1.0)
+        v = keep.tile([P, 4, B], F32, name="v")
         vr = keep.tile([P, 4, B], F32, name="vr")
-        nc.vector.tensor_scalar(out=vr[:], in0=v[:], scalar1=0.0, scalar2=1e-3, op0=ALU.max, op1=ALU.add)
         vl = keep.tile([P, 4, B], F32, name="vl")
         std = keep.tile([P, 4, B], F32, name="std")
 
@@ -175,19 +178,16 @@ def tile_hetxlhead_pa_kernel(tc, features, W_diag, b_diag, W_cls, b_cls, noise_d
                 warm(WARM_RUN)
             nc.vector.tensor_copy(out=wcg[:, 2 * i : 2 * i + 2].bitcast(F32), in_=xc[:].rearrange("p a u m -> p a m u"))
             if i == 1:
-                finish_std(0, 32)
-        finish_std(32, B)
+                nc.vector.tensor_tensor(out=v[:], in0=zt[:], in1=bd[:].unsqueeze(2).to_broadcast([P, 4, B]), op=ALU.add)
+                nc.vector.tensor_scalar(out=vr[:], in0=v[:], scalar1=0.0, scalar2=1e-3, op0=ALU.max, op1=ALU.add)
+        finish_std(0, 32)
         for h in range(2):
             nc.vector.quantize_mx(
                 out=wc_codes[:, h * 512 : (h + 1) * 512].bitcast(FP8X4),
                 scales=wc_scl[:, h * 512 : (h + 1) * 512],
                 in_=wcg[:, 4 * h : 4 * h + 4].rearrange("p a m k -> p (a m k)"),
             )
-        b15 = keep.tile([P, C], F32, name="b15")
-        for h in range(2):
-            pb = psum.tile([P, 512], F32, name="pb%d" % h, tag="o", bufs=4)
-            nc.tensor.matmul(out=pb[:], lhsT=ones[:], rhs=brow[:, h * 512 : (h + 1) * 512], start=True, stop=True)
-            nc.vector.tensor_scalar_mul(out=b15[:, h * 512 : (h + 1) * 512], in0=pb[:], scalar1=INV_T)
+        after_q = keep.tile([P, 1], U32, name="after_q")
 
         lT = {}
         tps = {}
@@ -200,11 +200,11 @@ def tile_hetxlhead_pa_kernel(tc, features, W_diag, b_diag, W_cls, b_cls, noise_d
         def turn_lr(j):
             lT[j] = psum.tile([P, 2, 2, P], F32, name="lT%d" % j, tag="lT")
             for g in range(2):
-                transpose_words(lT[j][:, g], l_words[j][:, g])
+                transpose_words(lT[j][:, :, g], l_words[j][:, g])
 
         def scale_noise(j, first, last):
             if first == 0:
-                tps[j] = work.tile([P, 4, 2, P], F32, name="tp%d" % j, tag="tp")
+                tps[j] = work.tile([P, 4, 2, P], F32, name="tp%d" % j, tag="tp", bufs=4)
             src = nT[j][:].bitcast(BF16).rearrange("p g u (r e) -> p g u r e", e=2)
             for i in range(first, last):
                 bl = i // 4
@@ -222,11 +222,10 @@ def tile_hetxlhead_pa_kernel(tc, features, W_diag, b_diag, W_cls, b_cls, noise_d
         def add_lr(j):
             pre = work.tile([P, 2, P, 4], BF16, name="pre%d" % j, tag="pre", align_bytes=64)
             pres[j] = pre
-            a = lT[j][:].bitcast(BF16).rearrange("p g u (r e) -> p g r u e", e=2)
-            c = tps[j][:].rearrange("p (u e) g r -> p g r u e", e=2)
-            o = pre[:].rearrange("p g r (u e) -> p g r u e", e=2)
-            for g in range(2):
-                nc.vector.tensor_tensor(out=o[:, g], in0=a[:, g], in1=c[:, g], op=ALU.add)
+            a = lT[j][:].bitcast(BF16).rearrange("p u g (r e) -> p (g r) u e", e=2)
+            c = tps[j][:].rearrange("p (u e) g r -> p (g r) u e", e=2)
+            o = pre[:].rearrange("p g r (u e) -> p (g r) u e", e=2)
+            nc.vector.tensor_tensor(out=o, in0=a, in1=c, op=ALU.add)
 
         def quantize(j):
             codes[j] = work.tile([P, 2 * P], U32, name="codes%d" % j, tag="codes", align_bytes=64)
@@ -234,6 +233,7 @@ def tile_hetxlhead_pa_kernel(tc, features, W_diag, b_diag, W_cls, b_cls, noise_d
             nc.vector.quantize_mx(
                 out=codes[j][:].bitcast(FP8X4), scales=scls[j][:], in_=pres[j][:].rearrange("p g r t -> p (g r t)")
             )
+            nc.gpsimd.tensor_copy(out=after_q[:], in_=codes[j][:, 0:1])
 
         def multiply(j, k):
             g = k // 2
@@ -265,20 +265,21 @@ def tile_hetxlhead_pa_kernel(tc, features, W_diag, b_diag, W_cls, b_cls, noise_d
                     out=dst, in0=obanks[(j, k)][:], scalar=INV_T, in1=b15[:, cols], op0=ALU.mult, op1=ALU.add
                 )
 
-        for step in range(NG + 2):
+        for step in range(NG + 3):
             jw = step
-            ja = step - 1
-            je = step - 2
+            ja = step - 2
+            je = step - 3
+            jl = step - 1
             do_w = jw < NG
             do_a = 0 <= ja < NG
             do_e = je >= 0
             last = je == NG - 1
             jn = step + 2
             loop_noise = LOOP_NOISE <= jn < NG
-            scalar_takes = (0,) if last else ((1, 3) if (je % 2 == 1 or step >= NG) else (3,))
+            scalar_takes = () if last else ((1, 3) if (je % 2 == 1 or jn >= NG) else (3,))
 
-            if do_w:
-                turn_lr(jw)
+            if 0 <= jl < NG:
+                turn_lr(jl)
             if loop_noise:
                 turn_noise(jn, "xn", 1)
             if step == 0:
@@ -290,7 +291,7 @@ def tile_hetxlhead_pa_kernel(tc, features, W_diag, b_diag, W_cls, b_cls, noise_d
             if step == 1:
                 for j in (6, 7):
                     turn_noise(j, "o", 4)
-            if step < NG + 1:
+            if step < NG + 2:
                 warm(WARM_RUN)
 
             if do_w:
@@ -300,18 +301,22 @@ def tile_hetxlhead_pa_kernel(tc, features, W_diag, b_diag, W_cls, b_cls, noise_d
                     copy_noise(j, False)
             if do_a:
                 add_lr(ja)
-            if step == 1:
+            if step == 2:
                 copy_noise(6, False)
             if do_e:
                 empty(je, 0, 0 in scalar_takes)
             if do_a:
                 quantize(ja)
                 multiply(ja, 0)
-            if step == 1:
+            if step == 2:
                 copy_noise(7, False)
+            if last:
+                nc.sync.dma_start(out=o_rows[:, je, 0, 0:512], in_=osbs[je][:, 0, 0:512])
             if do_e:
                 empty(je, 1, 1 in scalar_takes)
                 if last:
+                    nc.sync.dma_start(out=o_rows[:, je, 0, 512:C], in_=osbs[je][:, 0, 512:C])
+                elif je == NG - 2:
                     nc.sync.dma_start(out=o_rows[:, je, 0], in_=osbs[je][:, 0])
             if do_a:
                 multiply(ja, 1)
@@ -319,6 +324,8 @@ def tile_hetxlhead_pa_kernel(tc, features, W_diag, b_diag, W_cls, b_cls, noise_d
                 scale_noise(jw, CUTS[0], CUTS[1])
             if do_e:
                 empty(je, 3, 3 in scalar_takes)
+                if last:
+                    nc.sync.dma_start(out=o_rows[:, je, 1, 512:C], in_=osbs[je][:, 1, 512:C])
             if loop_noise:
                 copy_noise(jn, True)
             if do_e:
@@ -328,8 +335,12 @@ def tile_hetxlhead_pa_kernel(tc, features, W_diag, b_diag, W_cls, b_cls, noise_d
                 multiply(ja, 3)
             if do_w:
                 scale_noise(jw, CUTS[1], 32)
+            if step == 1:
+                finish_std(32, B)
             if do_e:
                 if last:
+                    nc.sync.dma_start(out=o_rows[:, je, 1, 0:512], in_=osbs[je][:, 1, 0:512])
+                elif je == NG - 2:
                     nc.sync.dma_start(out=o_rows[:, je, 1], in_=osbs[je][:, 1])
                 else:
                     nc.sync.dma_start(out=o_rows[:, je], in_=osbs[je][:])

@@ -292,7 +292,7 @@ def tile_hetxlhead_pa_kernel(tc, features, W_diag, b_diag, W_cls, b_cls, noise_d
                 for j in (6, 7):
                     turn_noise(j, "o", 4)
             if step < NG + 2:
-                warm(WARM_RUN)
+                warm(WARM_RUN if step < 3 else 1)
 
             if do_w:
                 scale_noise(jw, 0, CUTS[0])

@@ -276,7 +276,7 @@ def tile_hetxlhead_pa_kernel(tc, features, W_diag, b_diag, W_cls, b_cls, noise_d
             last = je == NG - 1
             jn = step + 2
             loop_noise = LOOP_NOISE <= jn < NG
-            scalar_takes = () if last else ((1, 3) if (je % 2 == 1 or jn >= NG) else (3,))
+            scalar_takes = () if last else (3,)
 
             if 0 <= jl < NG:
                 turn_lr(jl)

@@ -252,17 +252,17 @@ def tile_hetxlhead_pa_kernel(tc, features, W_diag, b_diag, W_cls, b_cls, noise_d
                 stop=True,
             )
 
-        def empty(j, k, on_scalar):
+        def empty(j, k, on_scalar, c0=0, c1=512):
             if j not in osbs:
                 osbs[j] = work.tile([P, 2, C], F32, name="osb%d" % j, tag="osb")
-            cols = slice((k % 2) * 512, (k % 2 + 1) * 512)
+            cols = slice((k % 2) * 512 + c0, (k % 2) * 512 + c1)
             dst = osbs[j][:, k // 2, cols]
             if on_scalar:
-                nc.scalar.activation(out=dst, in_=obanks[(j, k)][:], func=ACT.Copy, scale=INV_T)
+                nc.scalar.activation(out=dst, in_=obanks[(j, k)][:, c0:c1], func=ACT.Copy, scale=INV_T)
                 nc.gpsimd.tensor_tensor(out=dst, in0=dst, in1=b15[:, cols], op=ALU.add)
             else:
                 nc.vector.scalar_tensor_tensor(
-                    out=dst, in0=obanks[(j, k)][:], scalar=INV_T, in1=b15[:, cols], op0=ALU.mult, op1=ALU.add
+                    out=dst, in0=obanks[(j, k)][:, c0:c1], scalar=INV_T, in1=b15[:, cols], op0=ALU.mult, op1=ALU.add
                 )
 
         for step in range(NG + 3):
@@ -313,7 +313,12 @@ def tile_hetxlhead_pa_kernel(tc, features, W_diag, b_diag, W_cls, b_cls, noise_d
             if last:
                 nc.sync.dma_start(out=o_rows[:, je, 0, 0:512], in_=osbs[je][:, 0, 0:512])
             if do_e:
-                empty(je, 1, 1 in scalar_takes)
+                if last:
+                    empty(je, 1, False)
+                else:
+                    cut = 512 - (128 if loop_noise else 256)
+                    empty(je, 1, True, cut, 512)
+                    empty(je, 1, False, 0, cut)
                 if last:
                     nc.sync.dma_start(out=o_rows[:, je, 0, 512:C], in_=osbs[je][:, 0, 512:C])
                 elif je == NG - 2:

@@ -252,6 +252,14 @@ def tile_hetxlhead_pa_kernel(tc, features, W_diag, b_diag, W_cls, b_cls, noise_d
                 stop=True,
             )
 
+        def empty_unbiased(j, k, c0):
+            cols = slice((k % 2) * 512 + c0, (k % 2 + 1) * 512)
+            nc.scalar.activation(out=osbs[j][:, k // 2, cols], in_=obanks[(j, k)][:, c0:512], func=ACT.Copy, scale=INV_T)
+
+        def add_bias(j, c0):
+            dst = osbs[j][:, 1, c0:C]
+            nc.gpsimd.tensor_tensor(out=dst, in0=dst, in1=b15[:, c0:C], op=ALU.add)
+
         def empty(j, k, on_scalar, c0=0, c1=512):
             if j not in osbs:
                 osbs[j] = work.tile([P, 2, C], F32, name="osb%d" % j, tag="osb")
@@ -317,24 +325,27 @@ def tile_hetxlhead_pa_kernel(tc, features, W_diag, b_diag, W_cls, b_cls, noise_d
                     empty(je, 1, False)
                 else:
                     cut = 512 - (128 if loop_noise else 256)
-                    empty(je, 1, True, cut, 512)
-                    empty(je, 1, False, 0, cut)
+                    empty_unbiased(je, 2, cut)
+                    empty(je, 1, False)
                 if last:
                     nc.sync.dma_start(out=o_rows[:, je, 0, 512:C], in_=osbs[je][:, 0, 512:C])
-                elif je == NG - 2:
+                elif je >= NG - 6:
                     nc.sync.dma_start(out=o_rows[:, je, 0], in_=osbs[je][:, 0])
             if do_a:
                 multiply(ja, 1)
             if do_w:
                 scale_noise(jw, CUTS[0], CUTS[1])
             if do_e:
-                empty(je, 3, 3 in scalar_takes)
                 if last:
+                    empty(je, 3, False)
                     nc.sync.dma_start(out=o_rows[:, je, 1, 512:C], in_=osbs[je][:, 1, 512:C])
+                else:
+                    empty_unbiased(je, 3, 0)
+                    add_bias(je, cut)
             if loop_noise:
                 copy_noise(jn, True)
             if do_e:
-                empty(je, 2, 2 in scalar_takes)
+                empty(je, 2, False, 0, 512 if last else cut)
             if do_a:
                 multiply(ja, 2)
                 multiply(ja, 3)
@@ -345,7 +356,7 @@ def tile_hetxlhead_pa_kernel(tc, features, W_diag, b_diag, W_cls, b_cls, noise_d
             if do_e:
                 if last:
                     nc.sync.dma_start(out=o_rows[:, je, 1, 0:512], in_=osbs[je][:, 1, 0:512])
-                elif je == NG - 2:
+                elif je >= NG - 6:
                     nc.sync.dma_start(out=o_rows[:, je, 1], in_=osbs[je][:, 1])
                 else:
                     nc.sync.dma_start(out=o_rows[:, je], in_=osbs[je][:])

@@ -18,7 +18,8 @@ ZBANK = BF16
 NG = 16
 GB = 8
 INV_T = 1.0 / 1.5
-LOADS = (("n", 0, 2), ("w", 0, 0), ("n", 2, 2), ("n", 4, 4), ("l", 0, 2), ("l", 2, 2), ("n", 8, 4), ("l", 4, 4), ("n", 12, 4), ("l", 8, 4), ("l", 12, 4))
+BIG = 3.0e38
+LOADS = (("n", 0, 2), ("w", 0, 0), ("n", 2, 2), ("l", 0, 2), ("n", 4, 4), ("l", 2, 2), ("n", 8, 4), ("l", 4, 4), ("n", 12, 4), ("l", 8, 4), ("l", 12, 4))
 LOOP_NOISE = 8
 WARM_START = 4
 WARM_RUN = 2
@@ -39,13 +40,13 @@ def tile_hetxlhead_pa_kernel(tc, features, W_diag, b_diag, W_cls, b_cls, noise_d
 
         ident = keep.tile([P, P], F32, name="ident")
         make_identity(nc, ident[:])
+        warm_in = keep.tile([P, 2], F32, name="warm_in")
+        nc.vector.memset(warm_in[:], 0.0)
+        nc.scalar.activation(out=warm_in[:, 1:2], in_=warm_in[:, 0:1], func=ACT.Exp)
         brow = keep.tile([P, C], BF16, name="brow")
         nc.vector.memset(brow[:], 0.0)
         ones = keep.tile([P, P], BF16, name="ones")
         nc.vector.memset(ones[:], 1.0)
-        warm_in = keep.tile([P, 2], F32, name="warm_in")
-        nc.vector.memset(warm_in[:], 0.0)
-        nc.scalar.activation(out=warm_in[:, 1:2], in_=warm_in[:, 0:1], func=ACT.Exp)
 
         f_raw = keep.tile([P, D], BF16, name="f_raw")
         nc.sync.dma_start(out=f_raw[:], in_=features)
@@ -134,10 +135,6 @@ def tile_hetxlhead_pa_kernel(tc, features, W_diag, b_diag, W_cls, b_cls, noise_d
             pb = psum.tile([P, 512], F32, name="pb%d" % h, tag="o", bufs=4)
             nc.tensor.matmul(out=pb[:], lhsT=ones[:], rhs=brow[:, h * 512 : (h + 1) * 512], start=True, stop=True)
             nc.scalar.activation(out=b15[:, h * 512 : (h + 1) * 512], in_=pb[:], func=ACT.Copy, scale=INV_T)
-        for j in range(2):
-            turn_noise(j, "o", 4)
-            copy_noise(j, True)
-        warm(WARM_RUN)
 
         zt = psum.tile([P, 4, P], ZBANK, name="zt", tag="xn", bufs=1)
         for t in range(4):
@@ -152,19 +149,34 @@ def tile_hetxlhead_pa_kernel(tc, features, W_diag, b_diag, W_cls, b_cls, noise_d
                 stop=True,
             )
 
-        va = keep.tile([P, 4, B], F32, name="va")
-        for t in range(4):
-            nc.scalar.activation(out=va[:, t, :], in_=zt[:, t, :], func=ACT.Abs, bias=bd[:, t : t + 1])
         ve = keep.tile([P, 4, B], F32, name="ve")
-        nc.scalar.activation(out=ve[:], in_=va[:], func=ACT.Exp, scale=-1.0)
-        v = keep.tile([P, 4, B], F32, name="v")
-        vr = keep.tile([P, 4, B], F32, name="vr")
+        for t in range(4):
+            nc.scalar.activation(out=ve[:, t, :], in_=zt[:, t, :], func=ACT.Exp, bias=bd[:, t : t + 1])
+        v3 = keep.tile([P, 4, B], F32, name="v3")
+        nc.vector.scalar_tensor_tensor(
+            out=v3[:], in0=zt[:], scalar=1e-3, in1=bd[:].unsqueeze(2).to_broadcast([P, 4, B]), op0=ALU.add, op1=ALU.add
+        )
+        vc = keep.tile([P, 4, B], F32, name="vc")
         vl = keep.tile([P, 4, B], F32, name="vl")
         std = keep.tile([P, 4, B], F32, name="std")
 
+        def clamp_exp(b0, b1):
+            nc.vector.tensor_scalar(out=vc[:, :, b0:b1], in0=ve[:, :, b0:b1], scalar1=BIG, scalar2=None, op0=ALU.min)
+
+        def take_log(b0, b1):
+            nc.scalar.activation(out=vl[:, :, b0:b1], in_=vc[:, :, b0:b1], func=ACT.Ln, bias=1.0)
+
         def finish_std(b0, b1):
-            nc.scalar.activation(out=vl[:, :, b0:b1], in_=ve[:, :, b0:b1], func=ACT.Ln, bias=1.0)
-            nc.vector.tensor_tensor(out=std[:, :, b0:b1], in0=vr[:, :, b0:b1], in1=vl[:, :, b0:b1], op=ALU.add)
+            nc.vector.scalar_tensor_tensor(
+                out=std[:, :, b0:b1], in0=vl[:, :, b0:b1], scalar=1e-3, in1=v3[:, :, b0:b1], op0=ALU.add, op1=ALU.max
+            )
+
+        turn_noise(0, "o", 4)
+        copy_noise(0, False)
+        clamp_exp(0, 32)
+        take_log(0, 32)
+        turn_noise(1, "o", 4)
+        copy_noise(1, False)
 
         wc_words = wc_raw[:].bitcast(F32)
         wcg = keep.tile([P, 8, P, 4], BF16, name="wcg", align_bytes=64)
@@ -177,10 +189,9 @@ def tile_hetxlhead_pa_kernel(tc, features, W_diag, b_diag, W_cls, b_cls, noise_d
             if i % 2 == 1:
                 warm(WARM_RUN)
             nc.vector.tensor_copy(out=wcg[:, 2 * i : 2 * i + 2].bitcast(F32), in_=xc[:].rearrange("p a u m -> p a m u"))
-            if i == 1:
-                nc.vector.tensor_tensor(out=v[:], in0=zt[:], in1=bd[:].unsqueeze(2).to_broadcast([P, 4, B]), op=ALU.add)
-                nc.vector.tensor_scalar(out=vr[:], in0=v[:], scalar1=0.0, scalar2=1e-3, op0=ALU.max, op1=ALU.add)
-        finish_std(0, 32)
+            if i == 0:
+                clamp_exp(32, B)
+                finish_std(0, 32)
         for h in range(2):
             nc.vector.quantize_mx(
                 out=wc_codes[:, h * 512 : (h + 1) * 512].bitcast(FP8X4),
@@ -352,6 +363,7 @@ def tile_hetxlhead_pa_kernel(tc, features, W_diag, b_diag, W_cls, b_cls, noise_d
             if do_w:
                 scale_noise(jw, CUTS[1], 32)
             if step == 1:
+                take_log(32, B)
                 finish_std(32, B)
             if do_e:
                 if last:

@@ -20,8 +20,8 @@ GB = 8
 INV_T = 1.0 / 1.5
 BIG = 3.0e38
 LOADS = (("n", 0, 2), ("w", 0, 0), ("n", 2, 2), ("l", 0, 2), ("n", 4, 4), ("l", 2, 2), ("n", 8, 4), ("l", 4, 4), ("n", 12, 4), ("l", 8, 4), ("l", 12, 4))
-LOOP_NOISE = 8
-WARM_START = 4
+LOOP_NOISE = 4
+WARM_START = 3
 WARM_RUN = 2
 CUTS = (11, 21)
 
@@ -38,10 +38,12 @@ def tile_hetxlhead_pa_kernel(tc, features, W_diag, b_diag, W_cls, b_cls, noise_d
         l_rows = lr_samples.rearrange("b s d -> (b s) d").rearrange("(j r g) d -> r j g d", r=P, g=2)
         o_rows = out.rearrange("b s c -> (b s) c").rearrange("(j r g) c -> r j g c", r=P, g=2)
 
-        ident = keep.tile([P, P], F32, name="ident")
-        make_identity(nc, ident[:])
+        wz = keep.tile([P, P], F32, name="wz")
+        nc.vector.memset(wz[:], 1.0)
         warm_in = keep.tile([P, 2], F32, name="warm_in")
         nc.vector.memset(warm_in[:], 0.0)
+        ident = keep.tile([P, P], F32, name="ident")
+        make_identity(nc, ident[:])
         nc.scalar.activation(out=warm_in[:, 1:2], in_=warm_in[:, 0:1], func=ACT.Exp)
         brow = keep.tile([P, C], BF16, name="brow")
         nc.vector.memset(brow[:], 0.0)
@@ -79,7 +81,7 @@ def tile_hetxlhead_pa_kernel(tc, features, W_diag, b_diag, W_cls, b_cls, noise_d
 
         def warm(n):
             for i in range(n):
-                nc.tensor.matmul(out=dummy[:], lhsT=ident[:], rhs=ident[:], start=True, stop=True)
+                nc.tensor.matmul(out=dummy[:], lhsT=wz[:], rhs=wz[:], start=True, stop=True)
 
         def transpose_words(dst, words):
             for u in range(2):
@@ -161,7 +163,7 @@ def tile_hetxlhead_pa_kernel(tc, features, W_diag, b_diag, W_cls, b_cls, noise_d
         std = keep.tile([P, 4, B], F32, name="std")
 
         def clamp_exp(b0, b1):
-            nc.vector.tensor_scalar(out=vc[:, :, b0:b1], in0=ve[:, :, b0:b1], scalar1=BIG, scalar2=None, op0=ALU.min)
+            nc.gpsimd.tensor_scalar(out=vc[:, :, b0:b1], in0=ve[:, :, b0:b1], scalar1=BIG, scalar2=None, op0=ALU.min)
 
         def take_log(b0, b1):
             nc.scalar.activation(out=vl[:, :, b0:b1], in_=vc[:, :, b0:b1], func=ACT.Ln, bias=1.0)
@@ -304,31 +306,21 @@ def tile_hetxlhead_pa_kernel(tc, features, W_diag, b_diag, W_cls, b_cls, noise_d
             if step == 0:
                 for j in (2, 3):
                     turn_noise(j, "o", 4)
-                warm(WARM_RUN)
-                for j in (4, 5):
-                    turn_noise(j, "o", 4)
-            if step == 1:
-                for j in (6, 7):
-                    turn_noise(j, "o", 4)
             if step < NG + 2:
                 warm(WARM_RUN if step < 3 else 1)
 
             if do_w:
                 scale_noise(jw, 0, CUTS[0])
             if step == 0:
-                for j in (2, 3, 4, 5):
+                for j in (2, 3):
                     copy_noise(j, False)
             if do_a:
                 add_lr(ja)
-            if step == 2:
-                copy_noise(6, False)
             if do_e:
                 empty(je, 0, 0 in scalar_takes)
             if do_a:
                 quantize(ja)
                 multiply(ja, 0)
-            if step == 2:
-                copy_noise(7, False)
             if last:
                 nc.sync.dma_start(out=o_rows[:, je, 0, 0:512], in_=osbs[je][:, 0, 0:512])
             if do_e:

@@ -275,7 +275,7 @@ def tile_hetxlhead_pa_kernel(tc, features, W_diag, b_diag, W_cls, b_cls, noise_d
 
         def empty(j, k, on_scalar, c0=0, c1=512):
             if j not in osbs:
-                osbs[j] = work.tile([P, 2, C], F32, name="osb%d" % j, tag="osb")
+                osbs[j] = work.tile([P, 2, C], F32, name="osb%d" % j, tag="osb", bufs=6)
             cols = slice((k % 2) * 512 + c0, (k % 2) * 512 + c1)
             dst = osbs[j][:, k // 2, cols]
             if on_scalar:

@@ -327,7 +327,7 @@ def tile_hetxlhead_pa_kernel(tc, features, W_diag, b_diag, W_cls, b_cls, noise_d
                 if last:
                     empty(je, 1, False)
                 else:
-                    cut = 512 - (128 if loop_noise else 256)
+                    cut = 256
                     empty_unbiased(je, 2, cut)
                     empty(je, 1, False)
                 if last:

@@ -327,7 +327,7 @@ def tile_hetxlhead_pa_kernel(tc, features, W_diag, b_diag, W_cls, b_cls, noise_d
                 if last:
                     empty(je, 1, False)
                 else:
-                    cut = 256
+                    cut = 288
                     empty_unbiased(je, 2, cut)
                     empty(je, 1, False)
                 if last:

@@ -211,9 +211,10 @@ def tile_hetxlhead_pa_kernel(tc, features, W_diag, b_diag, W_cls, b_cls, noise_d
         osbs = {}
 
         def turn_lr(j):
-            lT[j] = psum.tile([P, 2, 2, P], F32, name="lT%d" % j, tag="lT")
+            lT[j] = psum.tile([P, 2, 32, 2, 4], F32, name="lT%d" % j, tag="lT")
             for g in range(2):
-                transpose_words(lT[j][:, :, g], l_words[j][:, g])
+                for u in range(2):
+                    nc.tensor.transpose(out=lT[j][:, g, :, u, :], in_=l_words[j][:, g][:, u : 256 : 2], identity=ident[:])
 
         def scale_noise(j, first, last):
             if first == 0:
@@ -235,9 +236,9 @@ def tile_hetxlhead_pa_kernel(tc, features, W_diag, b_diag, W_cls, b_cls, noise_d
         def add_lr(j):
             pre = work.tile([P, 2, P, 4], BF16, name="pre%d" % j, tag="pre", align_bytes=64)
             pres[j] = pre
-            a = lT[j][:].bitcast(BF16).rearrange("p u g (r e) -> p (g r) u e", e=2)
-            c = tps[j][:].rearrange("p (u e) g r -> p (g r) u e", e=2)
-            o = pre[:].rearrange("p g r (u e) -> p (g r) u e", e=2)
+            a = lT[j][:].bitcast(BF16).rearrange("p g c u (i e) -> p (g c) u e i", e=2)
+            c = tps[j][:].rearrange("p (u e) g (c i) -> p (g c) u e i", e=2, i=4)
+            o = pre[:].rearrange("p g (c i) (u e) -> p (g c) u e i", e=2, i=4)
             nc.vector.tensor_tensor(out=o, in0=a, in1=c, op=ALU.add)
 
         def quantize(j):

@@ -328,7 +328,7 @@ def tile_hetxlhead_pa_kernel(tc, features, W_diag, b_diag, W_cls, b_cls, noise_d
                 if last:
                     empty(je, 1, False)
                 else:
-                    cut = 288
+                    cut = 384
                     empty_unbiased(je, 2, cut)
                     empty(je, 1, False)
                 if last:

@@ -328,8 +328,9 @@ def tile_hetxlhead_pa_kernel(tc, features, W_diag, b_diag, W_cls, b_cls, noise_d
                 if last:
                     empty(je, 1, False)
                 else:
-                    cut = 384
-                    empty_unbiased(je, 2, cut)
+                    cut = 576 if loop_noise else 384
+                    if cut < 512:
+                        empty_unbiased(je, 2, cut)
                     empty(je, 1, False)
                 if last:
                     nc.sync.dma_start(out=o_rows[:, je, 0, 512:C], in_=osbs[je][:, 0, 512:C])
@@ -344,12 +345,14 @@ def tile_hetxlhead_pa_kernel(tc, features, W_diag, b_diag, W_cls, b_cls, noise_d
                     empty(je, 3, False)
                     nc.sync.dma_start(out=o_rows[:, je, 1, 512:C], in_=osbs[je][:, 1, 512:C])
                 else:
-                    empty_unbiased(je, 3, 0)
+                    empty_unbiased(je, 3, max(cut - 512, 0))
                     add_bias(je, cut)
             if loop_noise:
                 copy_noise(jn, True)
             if do_e:
-                empty(je, 2, False, 0, 512 if last else cut)
+                empty(je, 2, False, 0, 512 if last else min(cut, 512))
+                if not last and cut > 512:
+                    empty(je, 3, False, 0, cut - 512)
             if do_a:
                 multiply(ja, 2)
                 multiply(ja, 3)

@@ -307,8 +307,8 @@ def tile_hetxlhead_pa_kernel(tc, features, W_diag, b_diag, W_cls, b_cls, noise_d
             if step == 0:
                 for j in (2, 3):
                     turn_noise(j, "o", 4)
-            if step < NG + 2:
-                warm(WARM_RUN if step < 3 else 1)
+            if step < 3:
+                warm(WARM_RUN)
 
             if do_w:
                 scale_noise(jw, 0, CUTS[0])
@@ -328,7 +328,7 @@ def tile_hetxlhead_pa_kernel(tc, features, W_diag, b_diag, W_cls, b_cls, noise_d
                 if last:
                     empty(je, 1, False)
                 else:
-                    cut = 576 if loop_noise else 384
+                    cut = 512 if loop_noise else 384
                     if cut < 512:
                         empty_unbiased(je, 2, cut)
                     empty(je, 1, False)

@@ -23,6 +23,7 @@ LOADS = (("n", 0, 2), ("w", 0, 0), ("n", 2, 2), ("l", 0, 2), ("n", 4, 4), ("l", 
 LOOP_NOISE = 4
 WARM_START = 3
 WARM_RUN = 2
+POOL_FILL = 6
 CUTS = (11, 21)
 
 
@@ -107,6 +108,8 @@ def tile_hetxlhead_pa_kernel(tc, features, W_diag, b_diag, W_cls, b_cls, noise_d
         transpose_words(xf[:, 0], f_raw[:].bitcast(F32))
         fg = keep.tile([P, B, 4], BF16, name="fg", align_bytes=64)
         nc.vector.tensor_copy(out=fg[:].bitcast(F32), in_=xf[:, 0].rearrange("p u b -> p b u"))
+        fgf = keep.tile([P, B, 4], F32, name="fgf")
+        nc.gpsimd.tensor_scalar(out=fgf[:], in0=fg[:], scalar1=1.0, scalar2=0.0, op0=ALU.mult, op1=ALU.add)
         f_codes = keep.tile([P, B], U32, name="f_codes", align_bytes=64)
         f_scl = keep.tile([P, B], U8, name="f_scl", align_bytes=64)
         wd_codes = keep.tile([P, 4 * P], U32, name="wd_codes", align_bytes=64)
@@ -163,7 +166,7 @@ def tile_hetxlhead_pa_kernel(tc, features, W_diag, b_diag, W_cls, b_cls, noise_d
         std = keep.tile([P, 4, B], F32, name="std")
 
         def clamp_exp(b0, b1):
-            nc.gpsimd.tensor_scalar(out=vc[:, :, b0:b1], in0=ve[:, :, b0:b1], scalar1=BIG, scalar2=None, op0=ALU.min)
+            nc.gpsimd.tensor_scalar(out=vc[:, :, b0:b1], in0=ve[:, :, b0:b1], scalar1=BIG, scalar2=0.0, op0=ALU.min, op1=ALU.max)
 
         def take_log(b0, b1):
             nc.scalar.activation(out=vl[:, :, b0:b1], in_=vc[:, :, b0:b1], func=ACT.Ln, bias=1.0)
@@ -216,7 +219,7 @@ def tile_hetxlhead_pa_kernel(tc, features, W_diag, b_diag, W_cls, b_cls, noise_d
                 for u in range(2):
                     nc.tensor.transpose(out=lT[j][:, g, :, u, :], in_=l_words[j][:, g][:, u : 256 : 2], identity=ident[:])
 
-        def scale_noise(j, first, last):
+        def scale_noise(j, first, last, on_pool=False):
             if first == 0:
                 tps[j] = work.tile([P, 4, 2, P], F32, name="tp%d" % j, tag="tp", bufs=4)
             src = nT[j][:].bitcast(BF16).rearrange("p g u (r e) -> p g u r e", e=2)
@@ -225,13 +228,23 @@ def tile_hetxlhead_pa_kernel(tc, features, W_diag, b_diag, W_cls, b_cls, noise_d
                 t = i % 4
                 b = GB * j + bl
                 rr = slice(16 * bl, 16 * bl + 16)
-                nc.scalar.activation(
-                    out=tps[j][:, t, :, rr],
-                    in_=src[:, :, t // 2, rr, t % 2],
-                    func=ACT.Identity,
-                    bias=fg[:, b, t : t + 1],
-                    scale=std[:, t, b : b + 1],
-                )
+                if on_pool:
+                    nc.gpsimd.tensor_scalar(
+                        out=tps[j][:, t, :, rr],
+                        in0=src[:, :, t // 2, rr, t % 2],
+                        scalar1=std[:, t, b : b + 1],
+                        scalar2=fgf[:, b, t : t + 1],
+                        op0=ALU.mult,
+                        op1=ALU.add,
+                    )
+                else:
+                    nc.scalar.activation(
+                        out=tps[j][:, t, :, rr],
+                        in_=src[:, :, t // 2, rr, t % 2],
+                        func=ACT.Identity,
+                        bias=fg[:, b, t : t + 1],
+                        scale=std[:, t, b : b + 1],
+                    )
 
         def add_lr(j):
             pre = work.tile([P, 2, P, 4], BF16, name="pre%d" % j, tag="pre", align_bytes=64)
@@ -310,8 +323,10 @@ def tile_hetxlhead_pa_kernel(tc, features, W_diag, b_diag, W_cls, b_cls, noise_d
             if step < 3:
                 warm(WARM_RUN)
 
+            scalar_end = 32 - POOL_FILL if step < 3 else 32
             if do_w:
                 scale_noise(jw, 0, CUTS[0])
+                scale_noise(jw, scalar_end, 32, True)
             if step == 0:
                 for j in (2, 3):
                     copy_noise(j, False)
@@ -328,7 +343,7 @@ def tile_hetxlhead_pa_kernel(tc, features, W_diag, b_diag, W_cls, b_cls, noise_d
                 if last:
                     empty(je, 1, False)
                 else:
-                    cut = 512 if loop_noise else 384
+                    cut = 384
                     if cut < 512:
                         empty_unbiased(je, 2, cut)
                     empty(je, 1, False)
@@ -357,7 +372,7 @@ def tile_hetxlhead_pa_kernel(tc, features, W_diag, b_diag, W_cls, b_cls, noise_d
                 multiply(ja, 2)
                 multiply(ja, 3)
             if do_w:
-                scale_noise(jw, CUTS[1], 32)
+                scale_noise(jw, CUTS[1], scalar_end)
             if step == 1:
                 take_log(32, B)
                 finish_std(32, B)

@@ -320,8 +320,8 @@ def tile_hetxlhead_pa_kernel(tc, features, W_diag, b_diag, W_cls, b_cls, noise_d
             if step == 0:
                 for j in (2, 3):
                     turn_noise(j, "o", 4)
-            if step < 3:
-                warm(WARM_RUN)
+            if step < NG + 2:
+                warm(WARM_RUN if step < 3 else 1)
 
             scalar_end = 32 - POOL_FILL if step < 3 else 32
             if do_w:

@@ -343,7 +343,7 @@ def tile_hetxlhead_pa_kernel(tc, features, W_diag, b_diag, W_cls, b_cls, noise_d
                 if last:
                     empty(je, 1, False)
                 else:
-                    cut = 384
+                    cut = 512 if loop_noise else 384
                     if cut < 512:
                         empty_unbiased(je, 2, cut)
                     empty(je, 1, False)

@@ -214,7 +214,7 @@ def tile_hetxlhead_pa_kernel(tc, features, W_diag, b_diag, W_cls, b_cls, noise_d
         osbs = {}
 
         def turn_lr(j):
-            lT[j] = psum.tile([P, 2, 32, 2, 4], F32, name="lT%d" % j, tag="lT")
+            lT[j] = psum.tile([P, 2, 64, 2, 2], F32, name="lT%d" % j, tag="lT")
             for g in range(2):
                 for u in range(2):
                     nc.tensor.transpose(out=lT[j][:, g, :, u, :], in_=l_words[j][:, g][:, u : 256 : 2], identity=ident[:])
@@ -250,8 +250,8 @@ def tile_hetxlhead_pa_kernel(tc, features, W_diag, b_diag, W_cls, b_cls, noise_d
             pre = work.tile([P, 2, P, 4], BF16, name="pre%d" % j, tag="pre", align_bytes=64)
             pres[j] = pre
             a = lT[j][:].bitcast(BF16).rearrange("p g c u (i e) -> p (g c) u e i", e=2)
-            c = tps[j][:].rearrange("p (u e) g (c i) -> p (g c) u e i", e=2, i=4)
-            o = pre[:].rearrange("p g (c i) (u e) -> p (g c) u e i", e=2, i=4)
+            c = tps[j][:].rearrange("p (u e) g (c i) -> p (g c) u e i", e=2, i=2)
+            o = pre[:].rearrange("p g (c i) (u e) -> p (g c) u e i", e=2, i=2)
             nc.vector.tensor_tensor(out=o, in0=a, in1=c, op=ALU.add)
 
         def quantize(j):

@@ -323,10 +323,11 @@ def tile_hetxlhead_pa_kernel(tc, features, W_diag, b_diag, W_cls, b_cls, noise_d
             if step < NG + 2:
                 warm(WARM_RUN if step < 3 else 1)
 
-            scalar_end = 32 - POOL_FILL if step < 3 else 32
+            scalar_end = 32 - POOL_FILL if step < 3 else 32 - 1
             if do_w:
                 scale_noise(jw, 0, CUTS[0])
-                scale_noise(jw, scalar_end, 32, True)
+                if step < 3:
+                    scale_noise(jw, scalar_end, 32, True)
             if step == 0:
                 for j in (2, 3):
                     copy_noise(j, False)
@@ -338,17 +339,17 @@ def tile_hetxlhead_pa_kernel(tc, features, W_diag, b_diag, W_cls, b_cls, noise_d
                 quantize(ja)
                 multiply(ja, 0)
             if last:
-                nc.sync.dma_start(out=o_rows[:, je, 0, 0:512], in_=osbs[je][:, 0, 0:512])
+                nc.scalar.dma_start(out=o_rows[:, je, 0, 0:512], in_=osbs[je][:, 0, 0:512])
             if do_e:
                 if last:
                     empty(je, 1, False)
                 else:
-                    cut = 512 if loop_noise else 384
+                    cut = 448 if loop_noise else 384
                     if cut < 512:
                         empty_unbiased(je, 2, cut)
                     empty(je, 1, False)
                 if last:
-                    nc.sync.dma_start(out=o_rows[:, je, 0, 512:C], in_=osbs[je][:, 0, 512:C])
+                    nc.scalar.dma_start(out=o_rows[:, je, 0, 512:C], in_=osbs[je][:, 0, 512:C])
                 elif je >= NG - 6:
                     nc.sync.dma_start(out=o_rows[:, je, 0], in_=osbs[je][:, 0])
             if do_a:
@@ -362,6 +363,8 @@ def tile_hetxlhead_pa_kernel(tc, features, W_diag, b_diag, W_cls, b_cls, noise_d
                 else:
                     empty_unbiased(je, 3, max(cut - 512, 0))
                     add_bias(je, cut)
+                    if do_w:
+                        scale_noise(jw, scalar_end, 32, True)
             if loop_noise:
                 copy_noise(jn, True)
             if do_e:

@@ -344,7 +344,7 @@ def tile_hetxlhead_pa_kernel(tc, features, W_diag, b_diag, W_cls, b_cls, noise_d
                 if last:
                     empty(je, 1, False)
                 else:
-                    cut = 448 if loop_noise else 384
+                    cut = 448 if loop_noise else (320 if do_w else 256)
                     if cut < 512:
                         empty_unbiased(je, 2, cut)
                     empty(je, 1, False)

@@ -20,7 +20,7 @@ GB = 8
 INV_T = 1.0 / 1.5
 BIG = 3.0e38
 LOADS = (("n", 0, 2), ("w", 0, 0), ("n", 2, 2), ("l", 0, 2), ("n", 4, 4), ("l", 2, 2), ("n", 8, 4), ("l", 4, 4), ("n", 12, 4), ("l", 8, 4), ("l", 12, 4))
-LOOP_NOISE = 4
+LOOP_NOISE = 2
 WARM_START = 3
 WARM_RUN = 2
 POOL_FILL = 6
@@ -318,7 +318,7 @@ def tile_hetxlhead_pa_kernel(tc, features, W_diag, b_diag, W_cls, b_cls, noise_d
             if loop_noise:
                 turn_noise(jn, "xn", 1)
             if step == 0:
-                for j in (2, 3):
+                for j in range(2, LOOP_NOISE):
                     turn_noise(j, "o", 4)
             if step < NG + 2:
                 warm(WARM_RUN if step < 3 else 1)
@@ -329,7 +329,7 @@ def tile_hetxlhead_pa_kernel(tc, features, W_diag, b_diag, W_cls, b_cls, noise_d
                 if step < 3:
                     scale_noise(jw, scalar_end, 32, True)
             if step == 0:
-                for j in (2, 3):
+                for j in range(2, LOOP_NOISE):
                     copy_noise(j, False)
             if do_a:
                 add_lr(ja)
@@ -338,6 +338,8 @@ def tile_hetxlhead_pa_kernel(tc, features, W_diag, b_diag, W_cls, b_cls, noise_d
             if do_a:
                 quantize(ja)
                 multiply(ja, 0)
+            if step == 2:
+                finish_std(32, B)
             if last:
                 nc.scalar.dma_start(out=o_rows[:, je, 0, 0:512], in_=osbs[je][:, 0, 0:512])
             if do_e:
@@ -378,7 +380,6 @@ def tile_hetxlhead_pa_kernel(tc, features, W_diag, b_diag, W_cls, b_cls, noise_d
                 scale_noise(jw, CUTS[1], scalar_end)
             if step == 1:
                 take_log(32, B)
-                finish_std(32, B)
             if do_e:
                 if last:
                     nc.sync.dma_start(out=o_rows[:, je, 1, 0:512], in_=osbs[je][:, 1, 0:512])

@@ -367,7 +367,7 @@ def tile_hetxlhead_pa_kernel(tc, features, W_diag, b_diag, W_cls, b_cls, noise_d
                     add_bias(je, cut)
                     if do_w:
                         scale_noise(jw, scalar_end, 32, True)
-            if loop_noise:
+            if loop_noise and step >= 2:
                 copy_noise(jn, True)
             if do_e:
                 empty(je, 2, False, 0, 512 if last else min(cut, 512))
@@ -378,6 +378,8 @@ def tile_hetxlhead_pa_kernel(tc, features, W_diag, b_diag, W_cls, b_cls, noise_d
                 multiply(ja, 3)
             if do_w:
                 scale_noise(jw, CUTS[1], scalar_end)
+            if loop_noise and step < 2:
+                copy_noise(jn, True)
             if step == 1:
                 take_log(32, B)
             if do_e:

@@ -23,7 +23,7 @@ LOADS = (("n", 0, 2), ("w", 0, 0), ("n", 2, 2), ("l", 0, 2), ("n", 4, 4), ("l", 
 LOOP_NOISE = 2
 WARM_START = 3
 WARM_RUN = 2
-POOL_FILL = 6
+POOL_FILL = 4
 CUTS = (11, 21)
 
 
@@ -108,44 +108,43 @@ def tile_hetxlhead_pa_kernel(tc, features, W_diag, b_diag, W_cls, b_cls, noise_d
         transpose_words(xf[:, 0], f_raw[:].bitcast(F32))
         fg = keep.tile([P, B, 4], BF16, name="fg", align_bytes=64)
         nc.vector.tensor_copy(out=fg[:].bitcast(F32), in_=xf[:, 0].rearrange("p u b -> p b u"))
-        fgf = keep.tile([P, B, 4], F32, name="fgf")
-        nc.gpsimd.tensor_scalar(out=fgf[:], in0=fg[:], scalar1=1.0, scalar2=0.0, op0=ALU.mult, op1=ALU.add)
         f_codes = keep.tile([P, B], U32, name="f_codes", align_bytes=64)
         f_scl = keep.tile([P, B], U8, name="f_scl", align_bytes=64)
         wd_codes = keep.tile([P, 4 * P], U32, name="wd_codes", align_bytes=64)
         wd_scl = keep.tile([P, 4 * P], U8, name="wd_scl", align_bytes=64)
         wdg = []
-        for i in range(2):
-            xw = psum.tile([P, 2, 2, P], F32, name="xw%d" % i, tag="lT")
-            wd_words = wd_raw[i][:].bitcast(F32)
-            for a in range(2):
-                transpose_words(xw[:, a], wd_words[:, a])
-            wdg_half = keep.tile([P, 2, P, 4], BF16, name="wdg%d" % i, align_bytes=64)
-            wdg.append(wdg_half)
-            src = xw[:].rearrange("p a u m -> p a m u")
-            if i == 0:
-                nc.vector.tensor_copy(out=wdg_half[:].bitcast(F32), in_=src)
+        for t in range(4):
+            if t < 2:
+                xw = psum.tile([P, 2, P], F32, name="xw%d" % t, tag="lT")
+            else:
+                xw = psum.tile([P, 2, P], F32, name="xw%d" % t, tag="o", bufs=4)
+            transpose_words(xw[:], wd_raw[t // 2][:].bitcast(F32)[:, t % 2])
+            wdg_t = keep.tile([P, P, 4], BF16, name="wdg%d" % t, align_bytes=64)
+            wdg.append(wdg_t)
+            nc.scalar.copy(out=wdg_t[:].bitcast(F32), in_=xw[:].rearrange("p u m -> p m u"))
+            if t == 0:
                 nc.vector.quantize_mx(
                     out=f_codes[:].bitcast(FP8X4), scales=f_scl[:], in_=fg[:].rearrange("p b t -> p (b t)")
                 )
-            else:
-                nc.scalar.copy(out=wdg_half[:].bitcast(F32), in_=src)
-        for i in range(2):
-            cols = slice(2 * i * P, (2 * i + 2) * P)
-            nc.vector.quantize_mx(
-                out=wd_codes[:, cols].bitcast(FP8X4), scales=wd_scl[:, cols], in_=wdg[i][:].rearrange("p t m k -> p (t m k)")
-            )
-        b15 = keep.tile([P, C], F32, name="b15")
-        for h in range(2):
-            pb = psum.tile([P, 512], F32, name="pb%d" % h, tag="o", bufs=4)
-            nc.tensor.matmul(out=pb[:], lhsT=ones[:], rhs=brow[:, h * 512 : (h + 1) * 512], start=True, stop=True)
-            nc.scalar.activation(out=b15[:, h * 512 : (h + 1) * 512], in_=pb[:], func=ACT.Copy, scale=INV_T)
-
-        zt = psum.tile([P, 4, P], ZBANK, name="zt", tag="xn", bufs=1)
+        ve = keep.tile([P, 4, B], F32, name="ve")
+        v3 = keep.tile([P, 4, B], F32, name="v3")
         for t in range(4):
             cols = slice(t * P, (t + 1) * P)
+            nc.vector.quantize_mx(
+                out=wd_codes[:, cols].bitcast(FP8X4), scales=wd_scl[:, cols], in_=wdg[t][:].rearrange("p m k -> p (m k)")
+            )
+        zts = []
+        for t in range(4):
+            cols = slice(t * P, (t + 1) * P)
+            if t == 0:
+                zt = psum.tile([P, P], ZBANK, name="zt0", tag="xn", bufs=1)
+            elif t == 1:
+                zt = psum.tile([P, P], ZBANK, name="zt1", tag="o", bufs=4)
+            else:
+                zt = psum.tile([P, P], ZBANK, name="zt%d" % t, tag="lT")
+            zts.append(zt)
             nc.tensor.matmul_mx(
-                out=zt[:, t, :],
+                out=zt[:],
                 lhsT=wd_codes[:, cols].bitcast(FP8X4),
                 lhsT_scale=wd_scl[:, cols],
                 rhs=f_codes[:].bitcast(FP8X4),
@@ -153,14 +152,18 @@ def tile_hetxlhead_pa_kernel(tc, features, W_diag, b_diag, W_cls, b_cls, noise_d
                 start=True,
                 stop=True,
             )
-
-        ve = keep.tile([P, 4, B], F32, name="ve")
+            nc.scalar.activation(out=ve[:, t, :], in_=zt[:], func=ACT.Exp, bias=bd[:, t : t + 1])
         for t in range(4):
-            nc.scalar.activation(out=ve[:, t, :], in_=zt[:, t, :], func=ACT.Exp, bias=bd[:, t : t + 1])
-        v3 = keep.tile([P, 4, B], F32, name="v3")
-        nc.vector.scalar_tensor_tensor(
-            out=v3[:], in0=zt[:], scalar=1e-3, in1=bd[:].unsqueeze(2).to_broadcast([P, 4, B]), op0=ALU.add, op1=ALU.add
-        )
+            nc.vector.scalar_tensor_tensor(
+                out=v3[:, t, :], in0=zts[t][:], scalar=1e-3, in1=bd[:, t : t + 1].to_broadcast([P, B]), op0=ALU.add, op1=ALU.add
+            )
+        pb = psum.tile([P, C], BF16, name="pb", tag="o", bufs=4)
+        for h in range(2):
+            nc.tensor.matmul(out=pb[:, h * 512 : (h + 1) * 512], lhsT=ones[:], rhs=brow[:, h * 512 : (h + 1) * 512], start=True, stop=True)
+        bb = keep.tile([P, C], BF16, name="bb")
+        nc.vector.tensor_copy(out=bb[:], in_=pb[:])
+        b15 = keep.tile([P, C], F32, name="b15")
+        fgf = keep.tile([P, B, 4], F32, name="fgf")
         vc = keep.tile([P, 4, B], F32, name="vc")
         vl = keep.tile([P, 4, B], F32, name="vl")
         std = keep.tile([P, 4, B], F32, name="std")
@@ -176,33 +179,45 @@ def tile_hetxlhead_pa_kernel(tc, features, W_diag, b_diag, W_cls, b_cls, noise_d
                 out=std[:, :, b0:b1], in0=vl[:, :, b0:b1], scalar=1e-3, in1=v3[:, :, b0:b1], op0=ALU.add, op1=ALU.max
             )
 
-        turn_noise(0, "o", 4)
-        copy_noise(0, False)
         clamp_exp(0, 32)
         take_log(0, 32)
-        turn_noise(1, "o", 4)
-        copy_noise(1, False)
-
+        nc.gpsimd.tensor_scalar(out=fgf[:], in0=fg[:], scalar1=1.0, scalar2=0.0, op0=ALU.mult, op1=ALU.add)
+        clamp_exp(32, B)
         wc_words = wc_raw[:].bitcast(F32)
         wcg = keep.tile([P, 8, P, 4], BF16, name="wcg", align_bytes=64)
         wc_codes = keep.tile([P, C], U32, name="wc_codes", align_bytes=64)
         wc_scl = keep.tile([P, C], U8, name="wc_scl", align_bytes=64)
-        for i in range(4):
+
+        def turn_classes(i):
             xc = psum.tile([P, 2, 2, P], F32, name="xc%d" % i, tag="o", bufs=4)
             for a in range(2):
                 transpose_words(xc[:, a], wc_words[:, 2 * i + a])
-            if i % 2 == 1:
-                warm(WARM_RUN)
+            return xc
+
+        def copy_classes(i, xc):
             nc.vector.tensor_copy(out=wcg[:, 2 * i : 2 * i + 2].bitcast(F32), in_=xc[:].rearrange("p a u m -> p a m u"))
-            if i == 0:
-                clamp_exp(32, B)
-                finish_std(0, 32)
-        for h in range(2):
+
+        def quantize_classes(h):
             nc.vector.quantize_mx(
                 out=wc_codes[:, h * 512 : (h + 1) * 512].bitcast(FP8X4),
                 scales=wc_scl[:, h * 512 : (h + 1) * 512],
                 in_=wcg[:, 4 * h : 4 * h + 4].rearrange("p a m k -> p (a m k)"),
             )
+
+        turn_noise(0, "o", 4)
+        copy_noise(0, False)
+        turn_noise(1, "o", 4)
+        copy_noise(1, False)
+        finish_std(0, 32)
+        nc.gpsimd.tensor_scalar(out=b15[:], in0=bb[:], scalar1=INV_T, scalar2=0.0, op0=ALU.mult, op1=ALU.add)
+        copy_classes(0, turn_classes(0))
+        copy_classes(1, turn_classes(1))
+        warm(WARM_RUN)
+        copy_classes(2, turn_classes(2))
+        copy_classes(3, turn_classes(3))
+        warm(WARM_RUN)
+        quantize_classes(0)
+        quantize_classes(1)
         after_q = keep.tile([P, 1], U32, name="after_q")
 
         lT = {}
@@ -309,7 +324,7 @@ def tile_hetxlhead_pa_kernel(tc, features, W_diag, b_diag, W_cls, b_cls, noise_d
             do_a = 0 <= ja < NG
             do_e = je >= 0
             last = je == NG - 1
-            jn = step + 2
+            jn = step + 1
             loop_noise = LOOP_NOISE <= jn < NG
             scalar_takes = () if last else (3,)
 
@@ -321,7 +336,7 @@ def tile_hetxlhead_pa_kernel(tc, features, W_diag, b_diag, W_cls, b_cls, noise_d
                 for j in range(2, LOOP_NOISE):
                     turn_noise(j, "o", 4)
             if step < NG + 2:
-                warm(WARM_RUN if step < 3 else 1)
+                warm((0, 2, 2)[step] if step < 3 else 1)
 
             scalar_end = 32 - POOL_FILL if step < 3 else 32 - 1
             if do_w:

@@ -160,9 +160,8 @@ def tile_hetxlhead_pa_kernel(tc, features, W_diag, b_diag, W_cls, b_cls, noise_d
         pb = psum.tile([P, C], BF16, name="pb", tag="o", bufs=4)
         for h in range(2):
             nc.tensor.matmul(out=pb[:, h * 512 : (h + 1) * 512], lhsT=ones[:], rhs=brow[:, h * 512 : (h + 1) * 512], start=True, stop=True)
-        bb = keep.tile([P, C], BF16, name="bb")
-        nc.vector.tensor_copy(out=bb[:], in_=pb[:])
         b15 = keep.tile([P, C], F32, name="b15")
+        nc.vector.tensor_scalar(out=b15[:], in0=pb[:], scalar1=INV_T, scalar2=0.0, op0=ALU.mult, op1=ALU.add)
         fgf = keep.tile([P, B, 4], F32, name="fgf")
         vc = keep.tile([P, 4, B], F32, name="vc")
         vl = keep.tile([P, 4, B], F32, name="vl")
@@ -182,7 +181,6 @@ def tile_hetxlhead_pa_kernel(tc, features, W_diag, b_diag, W_cls, b_cls, noise_d
         clamp_exp(0, 32)
         take_log(0, 32)
         nc.gpsimd.tensor_scalar(out=fgf[:], in0=fg[:], scalar1=1.0, scalar2=0.0, op0=ALU.mult, op1=ALU.add)
-        clamp_exp(32, B)
         wc_words = wc_raw[:].bitcast(F32)
         wcg = keep.tile([P, 8, P, 4], BF16, name="wcg", align_bytes=64)
         wc_codes = keep.tile([P, C], U32, name="wc_codes", align_bytes=64)
@@ -207,9 +205,8 @@ def tile_hetxlhead_pa_kernel(tc, features, W_diag, b_diag, W_cls, b_cls, noise_d
         turn_noise(0, "o", 4)
         copy_noise(0, False)
         turn_noise(1, "o", 4)
-        copy_noise(1, False)
+        copy_noise(1, True)
         finish_std(0, 32)
-        nc.gpsimd.tensor_scalar(out=b15[:], in0=bb[:], scalar1=INV_T, scalar2=0.0, op0=ALU.mult, op1=ALU.add)
         copy_classes(0, turn_classes(0))
         copy_classes(1, turn_classes(1))
         warm(WARM_RUN)
@@ -343,6 +340,8 @@ def tile_hetxlhead_pa_kernel(tc, features, W_diag, b_diag, W_cls, b_cls, noise_d
                 scale_noise(jw, 0, CUTS[0])
                 if step < 3:
                     scale_noise(jw, scalar_end, 32, True)
+                if step == 0:
+                    clamp_exp(32, B)
             if step == 0:
                 for j in range(2, LOOP_NOISE):
                     copy_noise(j, False)

@@ -23,7 +23,7 @@ LOADS = (("n", 0, 2), ("w", 0, 0), ("n", 2, 2), ("l", 0, 2), ("n", 4, 4), ("l", 
 LOOP_NOISE = 2
 WARM_START = 3
 WARM_RUN = 2
-POOL_FILL = 4
+POOL_FILL = 3
 CUTS = (11, 21)
 
 
@@ -342,6 +342,7 @@ def tile_hetxlhead_pa_kernel(tc, features, W_diag, b_diag, W_cls, b_cls, noise_d
                     scale_noise(jw, scalar_end, 32, True)
                 if step == 0:
                     clamp_exp(32, B)
+                    nc.gpsimd.tensor_copy(out=after_q[:], in_=wc_codes[:, C - 1 : C])
             if step == 0:
                 for j in range(2, LOOP_NOISE):
                     copy_noise(j, False)
@@ -360,7 +361,7 @@ def tile_hetxlhead_pa_kernel(tc, features, W_diag, b_diag, W_cls, b_cls, noise_d
                 if last:
                     empty(je, 1, False)
                 else:
-                    cut = 448 if loop_noise else (320 if do_w else 256)
+                    cut = 416 if loop_noise else (320 if do_w else 256)
                     if cut < 512:
                         empty_unbiased(je, 2, cut)
                     empty(je, 1, False)

@@ -67,7 +67,7 @@ def tile_hetxlhead_pa_kernel(tc, features, W_diag, b_diag, W_cls, b_cls, noise_d
         l_words = {}
         for li, (what, j0, n) in enumerate(LOADS):
             if what == "w":
-                nc.sync.dma_start(out=wc_raw[:], in_=W_cls.rearrange("(a p) d -> p a d", p=P))
+                nc.sync.dma_start(out=wc_raw[:], in_=W_cls.rearrange("(p a) d -> p a d", a=8))
             else:
                 raw = keep.tile([P, n, 2, D], BF16, name="raw%d" % li)
                 rows = n_rows if what == "n" else l_rows
@@ -182,7 +182,7 @@ def tile_hetxlhead_pa_kernel(tc, features, W_diag, b_diag, W_cls, b_cls, noise_d
         take_log(0, 32)
         nc.gpsimd.tensor_scalar(out=fgf[:], in0=fg[:], scalar1=1.0, scalar2=0.0, op0=ALU.mult, op1=ALU.add)
         wc_words = wc_raw[:].bitcast(F32)
-        wcg = keep.tile([P, 8, P, 4], BF16, name="wcg", align_bytes=64)
+        wcg = keep.tile([P, P, 8, 4], BF16, name="wcg", align_bytes=64)
         wc_codes = keep.tile([P, C], U32, name="wc_codes", align_bytes=64)
         wc_scl = keep.tile([P, C], U8, name="wc_scl", align_bytes=64)
 
@@ -193,13 +193,13 @@ def tile_hetxlhead_pa_kernel(tc, features, W_diag, b_diag, W_cls, b_cls, noise_d
             return xc
 
         def copy_classes(i, xc):
-            nc.vector.tensor_copy(out=wcg[:, 2 * i : 2 * i + 2].bitcast(F32), in_=xc[:].rearrange("p a u m -> p a m u"))
+            nc.vector.tensor_copy(out=wcg[:, :, 2 * i : 2 * i + 2].bitcast(F32), in_=xc[:].rearrange("p a u m -> p m a u"))
 
         def quantize_classes(h):
             nc.vector.quantize_mx(
                 out=wc_codes[:, h * 512 : (h + 1) * 512].bitcast(FP8X4),
                 scales=wc_scl[:, h * 512 : (h + 1) * 512],
-                in_=wcg[:, 4 * h : 4 * h + 4].rearrange("p a m k -> p (a m k)"),
+                in_=wcg[:, 64 * h : 64 * h + 64].rearrange("p m a k -> p (m a k)"),
             )
 
         turn_noise(0, "o", 4)

@@ -157,11 +157,16 @@ def tile_hetxlhead_pa_kernel(tc, features, W_diag, b_diag, W_cls, b_cls, noise_d
             nc.vector.scalar_tensor_tensor(
                 out=v3[:, t, :], in0=zts[t][:], scalar=1e-3, in1=bd[:, t : t + 1].to_broadcast([P, B]), op0=ALU.add, op1=ALU.add
             )
-        pb = psum.tile([P, C], BF16, name="pb", tag="o", bufs=4)
+        pb = psum.tile([P, C], BF16, name="pb", tag="xn", bufs=1)
         for h in range(2):
             nc.tensor.matmul(out=pb[:, h * 512 : (h + 1) * 512], lhsT=ones[:], rhs=brow[:, h * 512 : (h + 1) * 512], start=True, stop=True)
         b15 = keep.tile([P, C], F32, name="b15")
-        nc.vector.tensor_scalar(out=b15[:], in0=pb[:], scalar1=INV_T, scalar2=0.0, op0=ALU.mult, op1=ALU.add)
+
+        def scale_bias(h):
+            cols = slice(h * 512, (h + 1) * 512)
+            nc.vector.tensor_scalar(out=b15[:, cols], in0=pb[:, cols], scalar1=INV_T, scalar2=0.0, op0=ALU.mult, op1=ALU.add)
+
+        scale_bias(0)
         fgf = keep.tile([P, B, 4], F32, name="fgf")
         vc = keep.tile([P, 4, B], F32, name="vc")
         vl = keep.tile([P, 4, B], F32, name="vl")
@@ -209,6 +214,7 @@ def tile_hetxlhead_pa_kernel(tc, features, W_diag, b_diag, W_cls, b_cls, noise_d
         finish_std(0, 32)
         copy_classes(0, turn_classes(0))
         copy_classes(1, turn_classes(1))
+        scale_bias(1)
         warm(WARM_RUN)
         copy_classes(2, turn_classes(2))
         copy_classes(3, turn_classes(3))

from contextlib import ExitStack

import concourse.mybir as mybir
from concourse.masks import make_identity

F32 = mybir.dt.float32
BF16 = mybir.dt.bfloat16
U32 = mybir.dt.uint32
U8 = mybir.dt.uint8
FP8X4 = mybir.dt.float8_e4m3fn_x4
ALU = mybir.AluOpType
ACT = mybir.ActivationFunctionType

B, S, D, C = 128, 32, 512, 1024
P = 128
FLOPS = 2 * B * S * D * C + 2 * B * D * D
ZBANK = BF16
NG = 16
GB = 8
INV_T = 1.0 / 1.5
BIG = 3.0e38
LOADS = (("n", 0, 2), ("w", 0, 0), ("n", 2, 2), ("l", 0, 2), ("n", 4, 4), ("l", 2, 2), ("n", 8, 4), ("l", 4, 4), ("n", 12, 4), ("l", 8, 4), ("l", 12, 4))
LOOP_NOISE = 2
WARM_START = 3
WARM_RUN = 2
POOL_FILL = 3
CUTS = (11, 21)


def tile_hetxlhead_pa_kernel(tc, features, W_diag, b_diag, W_cls, b_cls, noise_diag, lr_samples, out):
    nc = tc.nc
    with ExitStack() as ctx:
        keep = ctx.enter_context(tc.tile_pool(name="keep", bufs=1))
        work = ctx.enter_context(tc.tile_pool(name="work", bufs=3))
        psum = ctx.enter_context(tc.psum_pool(name="psum", bufs=2))
        ctx.enter_context(tc.manual_schedule())

        n_rows = noise_diag.rearrange("b s d -> (b s) d").rearrange("(j r g) d -> r j g d", r=P, g=2)
        l_rows = lr_samples.rearrange("b s d -> (b s) d").rearrange("(j r g) d -> r j g d", r=P, g=2)
        o_rows = out.rearrange("b s c -> (b s) c").rearrange("(j r g) c -> r j g c", r=P, g=2)

        wz = keep.tile([P, P], F32, name="wz")
        nc.vector.memset(wz[:], 1.0)
        warm_in = keep.tile([P, 2], F32, name="warm_in")
        nc.vector.memset(warm_in[:], 0.0)
        ident = keep.tile([P, P], F32, name="ident")
        make_identity(nc, ident[:])
        nc.scalar.activation(out=warm_in[:, 1:2], in_=warm_in[:, 0:1], func=ACT.Exp)
        brow = keep.tile([P, C], BF16, name="brow")
        nc.vector.memset(brow[:], 0.0)
        ones = keep.tile([P, P], BF16, name="ones")
        nc.vector.memset(ones[:], 1.0)

        f_raw = keep.tile([P, D], BF16, name="f_raw")
        nc.sync.dma_start(out=f_raw[:], in_=features)
        wd_rows = W_diag.rearrange("(m t) k -> m t k", t=4)
        wd_raw = []
        for i in range(2):
            wd_half = keep.tile([P, 2, D], BF16, name="wd_raw%d" % i)
            nc.sync.dma_start(out=wd_half[:], in_=wd_rows[:, 2 * i : 2 * i + 2])
            wd_raw.append(wd_half)
        nc.sync.dma_start(out=brow[0:1, :], in_=b_cls.rearrange("(o c) -> o c", o=1))
        bd = keep.tile([P, 4], BF16, name="bd")
        nc.sync.dma_start(out=bd[:], in_=b_diag.rearrange("(p t) -> p t", t=4))
        wc_raw = keep.tile([P, 8, D], BF16, name="wc_raw")
        n_words = {}
        l_words = {}
        for li, (what, j0, n) in enumerate(LOADS):
            if what == "w":
                nc.sync.dma_start(out=wc_raw[:], in_=W_cls.rearrange("(p a) d -> p a d", a=8))
            else:
                raw = keep.tile([P, n, 2, D], BF16, name="raw%d" % li)
                rows = n_rows if what == "n" else l_rows
                nc.sync.dma_start(out=raw[:], in_=rows[:, j0 : j0 + n])
                for i in range(n):
                    if what == "n":
                        n_words[j0 + i] = raw[:, i].bitcast(F32)
                    else:
                        l_words[j0 + i] = raw[:, i].bitcast(F32)

        dummy = psum.tile([P, P], F32, name="dummy", tag="dm", bufs=1)

        def warm(n):
            for i in range(n):
                nc.tensor.matmul(out=dummy[:], lhsT=wz[:], rhs=wz[:], start=True, stop=True)

        def transpose_words(dst, words):
            for u in range(2):
                nc.tensor.transpose(out=dst[:, u, :], in_=words[:, u : 256 : 2], identity=ident[:])

        nT = {}
        xns = {}

        def turn_noise(j, tag, bufs):
            xns[j] = psum.tile([P, 2, 2, P], F32, name="xn%d" % j, tag=tag, bufs=bufs)
            for g in range(2):
                transpose_words(xns[j][:, g], n_words[j][:, g])

        def copy_noise(j, on_scalar):
            nT[j] = keep.tile([P, 2, 2, P], F32, name="nT%d" % j)
            if on_scalar:
                nc.scalar.copy(out=nT[j][:], in_=xns[j][:])
            else:
                nc.vector.tensor_copy(out=nT[j][:], in_=xns[j][:])

        warm(WARM_START)
        xf = psum.tile([P, 2, 2, P], F32, name="xf", tag="xn", bufs=1)
        transpose_words(xf[:, 0], f_raw[:].bitcast(F32))
        fg = keep.tile([P, B, 4], BF16, name="fg", align_bytes=64)
        nc.vector.tensor_copy(out=fg[:].bitcast(F32), in_=xf[:, 0].rearrange("p u b -> p b u"))
        f_codes = keep.tile([P, B], U32, name="f_codes", align_bytes=64)
        f_scl = keep.tile([P, B], U8, name="f_scl", align_bytes=64)
        wd_codes = keep.tile([P, 4 * P], U32, name="wd_codes", align_bytes=64)
        wd_scl = keep.tile([P, 4 * P], U8, name="wd_scl", align_bytes=64)
        wdg = []
        for t in range(4):
            if t < 2:
                xw = psum.tile([P, 2, P], F32, name="xw%d" % t, tag="lT")
            else:
                xw = psum.tile([P, 2, P], F32, name="xw%d" % t, tag="o", bufs=4)
            transpose_words(xw[:], wd_raw[t // 2][:].bitcast(F32)[:, t % 2])
            wdg_t = keep.tile([P, P, 4], BF16, name="wdg%d" % t, align_bytes=64)
            wdg.append(wdg_t)
            nc.scalar.copy(out=wdg_t[:].bitcast(F32), in_=xw[:].rearrange("p u m -> p m u"))
            if t == 0:
                nc.vector.quantize_mx(
                    out=f_codes[:].bitcast(FP8X4), scales=f_scl[:], in_=fg[:].rearrange("p b t -> p (b t)")
                )
        ve = keep.tile([P, 4, B], F32, name="ve")
        v3 = keep.tile([P, 4, B], F32, name="v3")
        for t in range(4):
            cols = slice(t * P, (t + 1) * P)
            nc.vector.quantize_mx(
                out=wd_codes[:, cols].bitcast(FP8X4), scales=wd_scl[:, cols], in_=wdg[t][:].rearrange("p m k -> p (m k)")
            )
        zts = []
        for t in range(4):
            cols = slice(t * P, (t + 1) * P)
            if t == 0:
                zt = psum.tile([P, P], ZBANK, name="zt0", tag="xn", bufs=1)
            elif t == 1:
                zt = psum.tile([P, P], ZBANK, name="zt1", tag="o", bufs=4)
            else:
                zt = psum.tile([P, P], ZBANK, name="zt%d" % t, tag="lT")
            zts.append(zt)
            nc.tensor.matmul_mx(
                out=zt[:],
                lhsT=wd_codes[:, cols].bitcast(FP8X4),
                lhsT_scale=wd_scl[:, cols],
                rhs=f_codes[:].bitcast(FP8X4),
                rhs_scale=f_scl[:],
                start=True,
                stop=True,
            )
            nc.scalar.activation(out=ve[:, t, :], in_=zt[:], func=ACT.Exp, bias=bd[:, t : t + 1])
        for t in range(4):
            nc.vector.scalar_tensor_tensor(
                out=v3[:, t, :], in0=zts[t][:], scalar=1e-3, in1=bd[:, t : t + 1].to_broadcast([P, B]), op0=ALU.add, op1=ALU.add
            )
        pb = psum.tile([P, C], BF16, name="pb", tag="xn", bufs=1)
        for h in range(2):
            nc.tensor.matmul(out=pb[:, h * 512 : (h + 1) * 512], lhsT=ones[:], rhs=brow[:, h * 512 : (h + 1) * 512], start=True, stop=True)
        b15 = keep.tile([P, C], F32, name="b15")

        def scale_bias(h):
            cols = slice(h * 512, (h + 1) * 512)
            nc.vector.tensor_scalar(out=b15[:, cols], in0=pb[:, cols], scalar1=INV_T, scalar2=0.0, op0=ALU.mult, op1=ALU.add)

        scale_bias(0)
        fgf = keep.tile([P, B, 4], F32, name="fgf")
        vc = keep.tile([P, 4, B], F32, name="vc")
        vl = keep.tile([P, 4, B], F32, name="vl")
        std = keep.tile([P, 4, B], F32, name="std")

        def clamp_exp(b0, b1):
            nc.gpsimd.tensor_scalar(out=vc[:, :, b0:b1], in0=ve[:, :, b0:b1], scalar1=BIG, scalar2=0.0, op0=ALU.min, op1=ALU.max)

        def take_log(b0, b1):
            nc.scalar.activation(out=vl[:, :, b0:b1], in_=vc[:, :, b0:b1], func=ACT.Ln, bias=1.0)

        def finish_std(b0, b1):
            nc.vector.scalar_tensor_tensor(
                out=std[:, :, b0:b1], in0=vl[:, :, b0:b1], scalar=1e-3, in1=v3[:, :, b0:b1], op0=ALU.add, op1=ALU.max
            )

        clamp_exp(0, 32)
        take_log(0, 32)
        nc.gpsimd.tensor_scalar(out=fgf[:], in0=fg[:], scalar1=1.0, scalar2=0.0, op0=ALU.mult, op1=ALU.add)
        wc_words = wc_raw[:].bitcast(F32)
        wcg = keep.tile([P, P, 8, 4], BF16, name="wcg", align_bytes=64)
        wc_codes = keep.tile([P, C], U32, name="wc_codes", align_bytes=64)
        wc_scl = keep.tile([P, C], U8, name="wc_scl", align_bytes=64)

        def turn_classes(i):
            xc = psum.tile([P, 2, 2, P], F32, name="xc%d" % i, tag="o", bufs=4)
            for a in range(2):
                transpose_words(xc[:, a], wc_words[:, 2 * i + a])
            return xc

        def copy_classes(i, xc):
            nc.vector.tensor_copy(out=wcg[:, :, 2 * i : 2 * i + 2].bitcast(F32), in_=xc[:].rearrange("p a u m -> p m a u"))

        def quantize_classes(h):
            nc.vector.quantize_mx(
                out=wc_codes[:, h * 512 : (h + 1) * 512].bitcast(FP8X4),
                scales=wc_scl[:, h * 512 : (h + 1) * 512],
                in_=wcg[:, 64 * h : 64 * h + 64].rearrange("p m a k -> p (m a k)"),
            )

        turn_noise(0, "o", 4)
        copy_noise(0, False)
        turn_noise(1, "o", 4)
        copy_noise(1, True)
        finish_std(0, 32)
        copy_classes(0, turn_classes(0))
        copy_classes(1, turn_classes(1))
        scale_bias(1)
        warm(WARM_RUN)
        copy_classes(2, turn_classes(2))
        copy_classes(3, turn_classes(3))
        warm(WARM_RUN)
        quantize_classes(0)
        quantize_classes(1)
        after_q = keep.tile([P, 1], U32, name="after_q")

        lT = {}
        tps = {}
        pres = {}
        codes = {}
        scls = {}
        obanks = {}
        osbs = {}

        def turn_lr(j):
            lT[j] = psum.tile([P, 2, 64, 2, 2], F32, name="lT%d" % j, tag="lT")
            for g in range(2):
                for u in range(2):
                    nc.tensor.transpose(out=lT[j][:, g, :, u, :], in_=l_words[j][:, g][:, u : 256 : 2], identity=ident[:])

        def scale_noise(j, first, last, on_pool=False):
            if first == 0:
                tps[j] = work.tile([P, 4, 2, P], F32, name="tp%d" % j, tag="tp", bufs=4)
            src = nT[j][:].bitcast(BF16).rearrange("p g u (r e) -> p g u r e", e=2)
            for i in range(first, last):
                bl = i // 4
                t = i % 4
                b = GB * j + bl
                rr = slice(16 * bl, 16 * bl + 16)
                if on_pool:
                    nc.gpsimd.tensor_scalar(
                        out=tps[j][:, t, :, rr],
                        in0=src[:, :, t // 2, rr, t % 2],
                        scalar1=std[:, t, b : b + 1],
                        scalar2=fgf[:, b, t : t + 1],
                        op0=ALU.mult,
                        op1=ALU.add,
                    )
                else:
                    nc.scalar.activation(
                        out=tps[j][:, t, :, rr],
                        in_=src[:, :, t // 2, rr, t % 2],
                        func=ACT.Identity,
                        bias=fg[:, b, t : t + 1],
                        scale=std[:, t, b : b + 1],
                    )

        def add_lr(j):
            pre = work.tile([P, 2, P, 4], BF16, name="pre%d" % j, tag="pre", align_bytes=64)
            pres[j] = pre
            a = lT[j][:].bitcast(BF16).rearrange("p g c u (i e) -> p (g c) u e i", e=2)
            c = tps[j][:].rearrange("p (u e) g (c i) -> p (g c) u e i", e=2, i=2)
            o = pre[:].rearrange("p g (c i) (u e) -> p (g c) u e i", e=2, i=2)
            nc.vector.tensor_tensor(out=o, in0=a, in1=c, op=ALU.add)

        def quantize(j):
            codes[j] = work.tile([P, 2 * P], U32, name="codes%d" % j, tag="codes", align_bytes=64)
            scls[j] = work.tile([P, 2 * P], U8, name="scl%d" % j, tag="scl", align_bytes=64)
            nc.vector.quantize_mx(
                out=codes[j][:].bitcast(FP8X4), scales=scls[j][:], in_=pres[j][:].rearrange("p g r t -> p (g r t)")
            )
            nc.gpsimd.tensor_copy(out=after_q[:], in_=codes[j][:, 0:1])

        def multiply(j, k):
            g = k // 2
            h = k % 2
            rows = slice(g * P, (g + 1) * P)
            cols = slice(h * 512, (h + 1) * 512)
            ob = psum.tile([P, 512], F32, name="ob%d_%d" % (j, k), tag="o", bufs=4)
            obanks[(j, k)] = ob
            nc.tensor.matmul_mx(
                out=ob[:],
                lhsT=codes[j][:, rows].bitcast(FP8X4),
                lhsT_scale=scls[j][:, rows],
                rhs=wc_codes[:, cols].bitcast(FP8X4),
                rhs_scale=wc_scl[:, cols],
                start=True,
                stop=True,
            )

        def empty_unbiased(j, k, c0):
            cols = slice((k % 2) * 512 + c0, (k % 2 + 1) * 512)
            nc.scalar.activation(out=osbs[j][:, k // 2, cols], in_=obanks[(j, k)][:, c0:512], func=ACT.Copy, scale=INV_T)

        def add_bias(j, c0):
            dst = osbs[j][:, 1, c0:C]
            nc.gpsimd.tensor_tensor(out=dst, in0=dst, in1=b15[:, c0:C], op=ALU.add)

        def empty(j, k, on_scalar, c0=0, c1=512):
            if j not in osbs:
                osbs[j] = work.tile([P, 2, C], F32, name="osb%d" % j, tag="osb", bufs=6)
            cols = slice((k % 2) * 512 + c0, (k % 2) * 512 + c1)
            dst = osbs[j][:, k // 2, cols]
            if on_scalar:
                nc.scalar.activation(out=dst, in_=obanks[(j, k)][:, c0:c1], func=ACT.Copy, scale=INV_T)
                nc.gpsimd.tensor_tensor(out=dst, in0=dst, in1=b15[:, cols], op=ALU.add)
            else:
                nc.vector.scalar_tensor_tensor(
                    out=dst, in0=obanks[(j, k)][:, c0:c1], scalar=INV_T, in1=b15[:, cols], op0=ALU.mult, op1=ALU.add
                )

        for step in range(NG + 3):
            jw = step
            ja = step - 2
            je = step - 3
            jl = step - 1
            do_w = jw < NG
            do_a = 0 <= ja < NG
            do_e = je >= 0
            last = je == NG - 1
            jn = step + 1
            loop_noise = LOOP_NOISE <= jn < NG
            scalar_takes = () if last else (3,)

            if 0 <= jl < NG:
                turn_lr(jl)
            if loop_noise:
                turn_noise(jn, "xn", 1)
            if step == 0:
                for j in range(2, LOOP_NOISE):
                    turn_noise(j, "o", 4)
            if step < NG + 2:
                warm((0, 2, 2)[step] if step < 3 else 1)

            scalar_end = 32 - POOL_FILL if step < 3 else 32 - 1
            if do_w:
                scale_noise(jw, 0, CUTS[0])
                if step < 3:
                    scale_noise(jw, scalar_end, 32, True)
                if step == 0:
                    clamp_exp(32, B)
                    nc.gpsimd.tensor_copy(out=after_q[:], in_=wc_codes[:, C - 1 : C])
            if step == 0:
                for j in range(2, LOOP_NOISE):
                    copy_noise(j, False)
            if do_a:
                add_lr(ja)
            if do_e:
                empty(je, 0, 0 in scalar_takes)
            if do_a:
                quantize(ja)
                multiply(ja, 0)
            if step == 2:
                finish_std(32, B)
            if last:
                nc.scalar.dma_start(out=o_rows[:, je, 0, 0:512], in_=osbs[je][:, 0, 0:512])
            if do_e:
                if last:
                    empty(je, 1, False)
                else:
                    cut = 416 if loop_noise else (320 if do_w else 256)
                    if cut < 512:
                        empty_unbiased(je, 2, cut)
                    empty(je, 1, False)
                if last:
                    nc.scalar.dma_start(out=o_rows[:, je, 0, 512:C], in_=osbs[je][:, 0, 512:C])
                elif je >= NG - 6:
                    nc.sync.dma_start(out=o_rows[:, je, 0], in_=osbs[je][:, 0])
            if do_a:
                multiply(ja, 1)
            if do_w:
                scale_noise(jw, CUTS[0], CUTS[1])
            if do_e:
                if last:
                    empty(je, 3, False)
                    nc.sync.dma_start(out=o_rows[:, je, 1, 512:C], in_=osbs[je][:, 1, 512:C])
                else:
                    empty_unbiased(je, 3, max(cut - 512, 0))
                    add_bias(je, cut)
                    if do_w:
                        scale_noise(jw, scalar_end, 32, True)
            if loop_noise and step >= 2:
                copy_noise(jn, True)
            if do_e:
                empty(je, 2, False, 0, 512 if last else min(cut, 512))
                if not last and cut > 512:
                    empty(je, 3, False, 0, cut - 512)
            if do_a:
                multiply(ja, 2)
                multiply(ja, 3)
            if do_w:
                scale_noise(jw, CUTS[1], scalar_end)
            if loop_noise and step < 2:
                copy_noise(jn, True)
            if step == 1:
                take_log(32, B)
            if do_e:
                if last:
                    nc.sync.dma_start(out=o_rows[:, je, 1, 0:512], in_=osbs[je][:, 1, 0:512])
                elif je >= NG - 6:
                    nc.sync.dma_start(out=o_rows[:, je, 1], in_=osbs[je][:, 1])
                else:
                    nc.sync.dma_start(out=o_rows[:, je], in_=osbs[je][:])
